import numpy as np
import ml_dtypes


def mxq(x, axis, fmt="e4m3"):
    dtype, down = {"e4m3": (ml_dtypes.float8_e4m3fn, 7), "e5m2": (ml_dtypes.float8_e5m2, 14)}[fmt]
    v = np.moveaxis(np.asarray(x, np.float32).astype(ml_dtypes.bfloat16).astype(np.float64), axis, -1)
    blocks = v.reshape(v.shape[:-1] + (-1, 32))
    amax = np.abs(blocks).max(-1, keepdims=True)
    byte = np.maximum(np.where(amax > 0, np.frexp(amax)[1] - 1 + 127, 0) - down, 1)
    scale = np.exp2(byte - 127.0)
    codes = (blocks / scale).astype(np.float32).astype(dtype).astype(np.float64)
    return np.moveaxis((codes * scale).reshape(v.shape), -1, axis)


WIDE = False


def mx_kscale(k):
    if not WIDE:
        return np.ones(k)
    levels = np.array([10, -10, 5, -5, 0])
    a = np.random.permutation(np.resize(levels, k // 512 * 4)).reshape(k // 512, 4)
    idx = np.arange(k)
    return np.exp2(a[idx // 512, idx % 128 // 32])


BF16 = ml_dtypes.bfloat16


def bf(x):
    return np.asarray(x, np.float32).astype(BF16)


def f64(x):
    return np.asarray(x).astype(np.float64)


B, N, C, H, F = 16, 512, 512, 4, 2752
D = C // H
EPS = 1e-5


def rmsnorm(v, w):
    return v / np.sqrt(np.mean(v * v, axis=-1, keepdims=True) + EPS) * w


def setup_inputs():
    s = mx_kscale(C)
    return {"h": bf(np.random.standard_normal((B, N, C)) * s),
            "w_qk": bf(np.random.standard_normal((2 * C, C)) / np.sqrt(C) / s),
            "w_q_norm": bf(1.0 + 0.1 * np.random.standard_normal(D)),
            "w_k_norm": bf(1.0 + 0.1 * np.random.standard_normal(D))}


def reference(h, w_qk, w_q_norm, w_k_norm):
    qk = mxq(f64(h), 2, "e4m3") @ mxq(f64(w_qk), 1, "e4m3").T
    qk = qk.reshape(B, N, 2, H, D).transpose(2, 0, 3, 1, 4)
    q = rmsnorm(qk[0], f64(w_q_norm))
    k = rmsnorm(qk[1], f64(w_k_norm))
    a = (mxq(q, 2, "e4m3").transpose(0, 1, 3, 2) @ mxq(k, 2, "e4m3")) * D ** -0.5
    e = np.exp(a - a.max(-1, keepdims=True))
    return e / e.sum(-1, keepdims=True)

@@ -1,0 +1,246 @@
+from contextlib import ExitStack
+
+import concourse.mybir as mybir
+from concourse.masks import make_identity
+
+F32 = mybir.dt.float32
+BF16 = mybir.dt.bfloat16
+U32 = mybir.dt.uint32
+U8 = mybir.dt.uint8
+FP8X4 = mybir.dt.float8_e4m3fn_x4
+ACT = mybir.ActivationFunctionType
+ALU = mybir.AluOpType
+
+P = 128
+PACK = 4
+BATCH = 16
+TOKENS = 512
+CHANNELS = 512
+HEADS = 4
+HEAD_DIM = 128
+SIDES = 2
+EPS = 1e-5
+SOFTMAX_SCALE = HEAD_DIM**-0.5
+
+ROW_TILES = 4
+TOKEN_TILES = TOKENS // P
+SIDE_COLS = HEADS * HEAD_DIM
+QK_COLS = SIDES * SIDE_COLS
+WORDS = CHANNELS // 2
+
+FLOPS = 2 * BATCH * TOKENS * CHANNELS * QK_COLS + 2 * BATCH * HEADS * HEAD_DIM * HEAD_DIM * TOKENS
+
+
+def tile_transposedattentiontransformer_pa_t_kernel(tc, h, w_qk, w_q_norm, w_k_norm, out):
+    nc = tc.nc
+    with ExitStack() as ctx:
+        const = ctx.enter_context(tc.tile_pool(name="const", bufs=1))
+        rows_pool = ctx.enter_context(tc.tile_pool(name="rows", bufs=4))
+        stage = ctx.enter_context(tc.tile_pool(name="stage", bufs=2))
+        small = ctx.enter_context(tc.tile_pool(name="small", bufs=4))
+        soft = ctx.enter_context(tc.tile_pool(name="soft", bufs=3))
+        turned_pool = ctx.enter_context(tc.psum_pool(name="turned", bufs=2))
+        sums_pool = ctx.enter_context(tc.psum_pool(name="sums", bufs=6))
+        ctx.enter_context(tc.manual_schedule())
+
+        ident = const.tile([P, P], F32)
+        make_identity(nc, ident[:])
+        eps = const.tile([P, 1], F32)
+        nc.vector.memset(eps[:], EPS)
+        gains = const.tile([P, SIDES, HEAD_DIM], BF16)
+        nc.scalar.dma_start(out=gains[:, 0, :], in_=w_q_norm.partition_broadcast(P))
+        nc.scalar.dma_start(out=gains[:, 1, :], in_=w_k_norm.partition_broadcast(P))
+        squares = const.tile([P, HEAD_DIM], BF16)
+
+        w_codes = const.tile([P, QK_COLS], U32, align_bytes=64)
+        w_scales = const.tile([P, QK_COLS], U8, align_bytes=64)
+        qk_codes = const.tile([P, BATCH, QK_COLS], U32, align_bytes=64)
+        qk_scales = const.tile([P, BATCH, QK_COLS], U8, align_bytes=64)
+
+        def load_token_rows(b):
+            rows_sb = rows_pool.tile([P, ROW_TILES * CHANNELS], BF16, tag="rows")
+            nc.sync.dma_start(out=rows_sb[:], in_=h[b].rearrange("(p t) c -> p (t c)", t=ROW_TILES))
+            return rows_sb
+
+        def load_weight_rows(side):
+            rows_sb = rows_pool.tile([P, ROW_TILES * CHANNELS], BF16, tag="rows")
+            nc.sync.dma_start(
+                out=rows_sb[:].rearrange("p (r c) -> p r c", r=ROW_TILES),
+                in_=w_qk[side * SIDE_COLS : (side + 1) * SIDE_COLS, :].rearrange("(r p) c -> p r c", p=P),
+            )
+            return rows_sb
+
+        def transpose_rows(rows_sb):
+            words = rows_sb[:].bitcast(F32)
+            banks = []
+            for n in range(2):
+                turned = turned_pool.tile([P, 4, P], F32, tag="turned")
+                for i in range(4):
+                    block = 4 * n + i
+                    nc.tensor.transpose(turned[:, i, :], words[:, block * P : (block + 1) * P], ident[:])
+                banks.append(turned)
+            return banks
+
+        def gather_words(banks):
+            grouped = stage.tile([P, ROW_TILES * P * PACK], BF16, tag="grouped_rows", align_bytes=64)
+            pairs = grouped[:].bitcast(F32).rearrange("p (n r k u) -> p n r k u", n=2, r=2, u=2)
+            nc.scalar.copy(out=pairs[:, 0], in_=banks[0][:].rearrange("p (r u) k -> p r k u", u=2))
+            nc.vector.tensor_copy(out=pairs[:, 1], in_=banks[1][:].rearrange("p (r u) k -> p r k u", u=2))
+            return grouped
+
+        def quantise_rows(grouped, codes, scales):
+            nc.vector.quantize_mx(out=codes.bitcast(FP8X4), scales=scales, in_=grouped[:])
+
+        def new_token_codes():
+            h_codes = stage.tile([P, TOKENS], U32, tag="h_codes", align_bytes=64)
+            h_scales = stage.tile([P, TOKENS], U8, tag="h_scales", align_bytes=64)
+            return h_codes, h_scales
+
+        def project(h_codes, h_scales, t):
+            token_cols = slice(t * P, (t + 1) * P)
+            raw = []
+            for side in range(SIDES):
+                side_cols = slice(side * SIDE_COLS, (side + 1) * SIDE_COLS)
+                sums = sums_pool.tile([P, SIDE_COLS], F32, tag="sums")
+                nc.tensor.matmul_mx(
+                    out=sums[:],
+                    lhsT=h_codes[:, token_cols].bitcast(FP8X4),
+                    lhsT_scale=h_scales[:, token_cols],
+                    rhs=w_codes[:, side_cols].bitcast(FP8X4),
+                    rhs_scale=w_scales[:, side_cols],
+                    start=True,
+                    stop=True,
+                )
+                raw.append(sums)
+            return raw
+
+        def measure(raw):
+            sumsq = small.tile([P, SIDES * HEADS], F32, tag="sumsq")
+            for side in range(SIDES):
+                for g in range(HEADS):
+                    nc.scalar.activation(
+                        out=squares[:],
+                        in_=raw[side][:, g * HEAD_DIM : (g + 1) * HEAD_DIM],
+                        func=ACT.Square,
+                        accum_out=sumsq[:, side * HEADS + g : side * HEADS + g + 1],
+                    )
+            rms = small.tile([P, SIDES * HEADS], F32, tag="rms")
+            nc.scalar.activation(out=rms[:], in_=sumsq[:], func=ACT.Sqrt, scale=1.0 / HEAD_DIM, bias=eps[:])
+            return rms
+
+        def normalise(raw, rms, normed_rows):
+            inv_rms = small.tile([P, SIDES * HEADS], F32, tag="inv_rms")
+            nc.vector.reciprocal(out=inv_rms[:], in_=rms[:])
+            for side in range(SIDES):
+                for g in range(HEADS):
+                    nc.vector.scalar_tensor_tensor(
+                        out=normed_rows[:, side * SIDE_COLS + g * HEAD_DIM : side * SIDE_COLS + (g + 1) * HEAD_DIM],
+                        in0=raw[side][:, g * HEAD_DIM : (g + 1) * HEAD_DIM],
+                        scalar=inv_rms[:, side * HEADS + g : side * HEADS + g + 1],
+                        in1=gains[:, side, :],
+                        op0=ALU.mult,
+                        op1=ALU.mult,
+                    )
+
+        def regroup(normed):
+            grouped = stage.tile([P, QK_COLS, PACK], BF16, tag="grouped_qk", align_bytes=64)
+            for side in range(SIDES):
+                side_cols = slice(side * SIDE_COLS, (side + 1) * SIDE_COLS)
+                nc.gpsimd.tensor_scalar(
+                    out=grouped[:, side_cols, :],
+                    in0=normed[:, :, side_cols].rearrange("p t c -> p c t"),
+                    scalar1=1.0,
+                    scalar2=0.0,
+                    op0=ALU.mult,
+                    op1=ALU.add,
+                )
+            return grouped
+
+        def quantise_qk(grouped, b):
+            nc.vector.quantize_mx(
+                out=qk_codes[:, b, :].bitcast(FP8X4),
+                scales=qk_scales[:, b, :],
+                in_=grouped[:].rearrange("p c t -> p (c t)"),
+            )
+
+        def scores(b):
+            att = sums_pool.tile([P, HEADS, HEAD_DIM], F32, tag="sums")
+            for g in range(HEADS):
+                q_cols = slice(g * HEAD_DIM, (g + 1) * HEAD_DIM)
+                k_cols = slice(SIDE_COLS + g * HEAD_DIM, SIDE_COLS + (g + 1) * HEAD_DIM)
+                nc.tensor.matmul_mx(
+                    out=att[:, g, :],
+                    lhsT=qk_codes[:, b, q_cols].bitcast(FP8X4),
+                    lhsT_scale=qk_scales[:, b, q_cols],
+                    rhs=qk_codes[:, b, k_cols].bitcast(FP8X4),
+                    rhs_scale=qk_scales[:, b, k_cols],
+                    start=True,
+                    stop=True,
+                )
+            top = small.tile([P, HEADS], F32, tag="top")
+            nc.vector.tensor_reduce(out=top[:], in_=att[:], axis=mybir.AxisListType.X, op=ALU.max)
+            shift = small.tile([P, HEADS], F32, tag="shift")
+            nc.vector.tensor_scalar_mul(out=shift[:], in0=top[:], scalar1=-SOFTMAX_SCALE)
+            return att, shift
+
+        def exponentials(att, shift):
+            weights = soft.tile([P, HEADS, HEAD_DIM], F32, tag="weights")
+            total = small.tile([P, HEADS], F32, tag="total")
+            for g in range(HEADS):
+                nc.scalar.activation(
+                    out=weights[:, g, :],
+                    in_=att[:, g, :],
+                    func=ACT.Exp,
+                    scale=SOFTMAX_SCALE,
+                    bias=shift[:, g : g + 1],
+                    accum_out=total[:, g : g + 1],
+                )
+            return weights, total
+
+        def divide_and_store(weights, total, b):
+            inv_total = small.tile([P, HEADS], F32, tag="inv_total")
+            nc.vector.reciprocal(out=inv_total[:], in_=total[:])
+            for g in range(HEADS):
+                nc.vector.tensor_scalar_mul(out=weights[:, g, :], in0=weights[:, g, :], scalar1=inv_total[:, g : g + 1])
+            nc.sync.dma_start(out=out[b].rearrange("g d e -> d g e"), in_=weights[:])
+
+        token_rows = {0: load_token_rows(0)}
+        weight_rows = [load_weight_rows(side) for side in range(SIDES)]
+        token_rows[1] = load_token_rows(1)
+
+        token_codes = {0: new_token_codes()}
+        quantise_rows(gather_words(transpose_rows(token_rows[0])), token_codes[0][0][:], token_codes[0][1][:])
+        for side in range(SIDES):
+            side_cols = slice(side * SIDE_COLS, (side + 1) * SIDE_COLS)
+            quantise_rows(gather_words(transpose_rows(weight_rows[side])), w_codes[:, side_cols], w_scales[:, side_cols])
+
+        grouped_qk = {}
+        for b in range(BATCH):
+            if b + 2 < BATCH:
+                token_rows[b + 2] = load_token_rows(b + 2)
+            h_codes, h_scales = token_codes[b]
+            normed = stage.tile([P, TOKEN_TILES, QK_COLS], BF16, tag="normed")
+            for t in range(TOKEN_TILES):
+                raw = project(h_codes, h_scales, t)
+                rms = measure(raw)
+                if b + 1 < BATCH and t == 0:
+                    banks = transpose_rows(token_rows[b + 1])
+                if b + 1 < BATCH and t == 1:
+                    grouped_rows = gather_words(banks)
+                normalise(raw, rms, normed[:, t, :])
+                if b + 1 < BATCH and t == 2:
+                    token_codes[b + 1] = new_token_codes()
+                    quantise_rows(grouped_rows, token_codes[b + 1][0][:], token_codes[b + 1][1][:])
+            grouped_qk[b] = regroup(normed)
+            if b > 0:
+                quantise_qk(grouped_qk[b - 1], b - 1)
+
+        waiting = {0: scores(0)}
+        for b in range(BATCH):
+            if b + 1 == BATCH - 1:
+                quantise_qk(grouped_qk[b + 1], b + 1)
+            if b + 1 < BATCH:
+                waiting[b + 1] = scores(b + 1)
+            att, shift = waiting[b]
+            weights, total = exponentials(att, shift)
+            divide_and_store(weights, total, b)

@@ -26,7 +26,7 @@ ROW_TILES = 4
 TOKEN_TILES = TOKENS // P
 SIDE_COLS = HEADS * HEAD_DIM
 QK_COLS = SIDES * SIDE_COLS
-WORDS = CHANNELS // 2
+SUM_BANKS = 6
 
 FLOPS = 2 * BATCH * TOKENS * CHANNELS * QK_COLS + 2 * BATCH * HEADS * HEAD_DIM * HEAD_DIM * TOKENS
 
@@ -35,13 +35,15 @@ def tile_transposedattentiontransformer_pa_t_kernel(tc, h, w_qk, w_q_norm, w_k_n
     nc = tc.nc
     with ExitStack() as ctx:
         const = ctx.enter_context(tc.tile_pool(name="const", bufs=1))
-        rows_pool = ctx.enter_context(tc.tile_pool(name="rows", bufs=4))
-        stage = ctx.enter_context(tc.tile_pool(name="stage", bufs=2))
-        small = ctx.enter_context(tc.tile_pool(name="small", bufs=4))
-        soft = ctx.enter_context(tc.tile_pool(name="soft", bufs=3))
-        turned_pool = ctx.enter_context(tc.psum_pool(name="turned", bufs=2))
-        sums_pool = ctx.enter_context(tc.psum_pool(name="sums", bufs=6))
+        sbuf = ctx.enter_context(tc.tile_pool(name="sbuf", bufs=1))
+        psum = ctx.enter_context(tc.psum_pool(name="psum", bufs=1))
         ctx.enter_context(tc.manual_schedule())
+
+        def sbuf_ring(label, index, depth, shape, dtype):
+            return sbuf.tile(shape, dtype, name=label, tag="%s_%d" % (label, index % depth), align_bytes=64)
+
+        def psum_ring(label, index, depth, shape):
+            return psum.tile(shape, F32, name=label, tag="%s_%d" % (label, index % depth))
 
         ident = const.tile([P, P], F32)
         make_identity(nc, ident[:])
@@ -58,12 +60,12 @@ def tile_transposedattentiontransformer_pa_t_kernel(tc, h, w_qk, w_q_norm, w_k_n
         qk_scales = const.tile([P, BATCH, QK_COLS], U8, align_bytes=64)
 
         def load_token_rows(b):
-            rows_sb = rows_pool.tile([P, ROW_TILES * CHANNELS], BF16, tag="rows")
+            rows_sb = sbuf_ring("token_rows", b, 3, [P, ROW_TILES * CHANNELS], BF16)
             nc.sync.dma_start(out=rows_sb[:], in_=h[b].rearrange("(p t) c -> p (t c)", t=ROW_TILES))
             return rows_sb
 
         def load_weight_rows(side):
-            rows_sb = rows_pool.tile([P, ROW_TILES * CHANNELS], BF16, tag="rows")
+            rows_sb = sbuf_ring("weight_rows", side, SIDES, [P, ROW_TILES * CHANNELS], BF16)
             nc.sync.dma_start(
                 out=rows_sb[:].rearrange("p (r c) -> p r c", r=ROW_TILES),
                 in_=w_qk[side * SIDE_COLS : (side + 1) * SIDE_COLS, :].rearrange("(r p) c -> p r c", p=P),
@@ -74,15 +76,15 @@ def tile_transposedattentiontransformer_pa_t_kernel(tc, h, w_qk, w_q_norm, w_k_n
             words = rows_sb[:].bitcast(F32)
             banks = []
             for n in range(2):
-                turned = turned_pool.tile([P, 4, P], F32, tag="turned")
+                turned = psum_ring("turned", n, 2, [P, 4, P])
                 for i in range(4):
                     block = 4 * n + i
                     nc.tensor.transpose(turned[:, i, :], words[:, block * P : (block + 1) * P], ident[:])
                 banks.append(turned)
             return banks
 
-        def gather_words(banks):
-            grouped = stage.tile([P, ROW_TILES * P * PACK], BF16, tag="grouped_rows", align_bytes=64)
+        def gather_words(banks, call):
+            grouped = sbuf_ring("grouped_rows", call, 2, [P, ROW_TILES * P * PACK], BF16)
             pairs = grouped[:].bitcast(F32).rearrange("p (n r k u) -> p n r k u", n=2, r=2, u=2)
             nc.scalar.copy(out=pairs[:, 0], in_=banks[0][:].rearrange("p (r u) k -> p r k u", u=2))
             nc.vector.tensor_copy(out=pairs[:, 1], in_=banks[1][:].rearrange("p (r u) k -> p r k u", u=2))
@@ -91,17 +93,17 @@ def tile_transposedattentiontransformer_pa_t_kernel(tc, h, w_qk, w_q_norm, w_k_n
         def quantise_rows(grouped, codes, scales):
             nc.vector.quantize_mx(out=codes.bitcast(FP8X4), scales=scales, in_=grouped[:])
 
-        def new_token_codes():
-            h_codes = stage.tile([P, TOKENS], U32, tag="h_codes", align_bytes=64)
-            h_scales = stage.tile([P, TOKENS], U8, tag="h_scales", align_bytes=64)
+        def new_token_codes(b):
+            h_codes = sbuf_ring("h_codes", b, 2, [P, TOKENS], U32)
+            h_scales = sbuf_ring("h_scales", b, 2, [P, TOKENS], U8)
             return h_codes, h_scales
 
-        def project(h_codes, h_scales, t):
+        def project(h_codes, h_scales, t, step):
             token_cols = slice(t * P, (t + 1) * P)
             raw = []
             for side in range(SIDES):
                 side_cols = slice(side * SIDE_COLS, (side + 1) * SIDE_COLS)
-                sums = sums_pool.tile([P, SIDE_COLS], F32, tag="sums")
+                sums = psum_ring("sums", SIDES * step + side, SUM_BANKS, [P, SIDE_COLS])
                 nc.tensor.matmul_mx(
                     out=sums[:],
                     lhsT=h_codes[:, token_cols].bitcast(FP8X4),
@@ -114,8 +116,8 @@ def tile_transposedattentiontransformer_pa_t_kernel(tc, h, w_qk, w_q_norm, w_k_n
                 raw.append(sums)
             return raw
 
-        def measure(raw):
-            sumsq = small.tile([P, SIDES * HEADS], F32, tag="sumsq")
+        def measure(raw, step):
+            sumsq = sbuf_ring("sumsq", step, 4, [P, SIDES * HEADS], F32)
             for side in range(SIDES):
                 for g in range(HEADS):
                     nc.scalar.activation(
@@ -124,12 +126,12 @@ def tile_transposedattentiontransformer_pa_t_kernel(tc, h, w_qk, w_q_norm, w_k_n
                         func=ACT.Square,
                         accum_out=sumsq[:, side * HEADS + g : side * HEADS + g + 1],
                     )
-            rms = small.tile([P, SIDES * HEADS], F32, tag="rms")
+            rms = sbuf_ring("rms", step, 4, [P, SIDES * HEADS], F32)
             nc.scalar.activation(out=rms[:], in_=sumsq[:], func=ACT.Sqrt, scale=1.0 / HEAD_DIM, bias=eps[:])
             return rms
 
-        def normalise(raw, rms, normed_rows):
-            inv_rms = small.tile([P, SIDES * HEADS], F32, tag="inv_rms")
+        def normalise(raw, rms, normed_rows, step):
+            inv_rms = sbuf_ring("inv_rms", step, 4, [P, SIDES * HEADS], F32)
             nc.vector.reciprocal(out=inv_rms[:], in_=rms[:])
             for side in range(SIDES):
                 for g in range(HEADS):
@@ -142,17 +144,13 @@ def tile_transposedattentiontransformer_pa_t_kernel(tc, h, w_qk, w_q_norm, w_k_n
                         op1=ALU.mult,
                     )
 
-        def regroup(normed):
-            grouped = stage.tile([P, QK_COLS, PACK], BF16, tag="grouped_qk", align_bytes=64)
+        def regroup(normed, b):
+            grouped = sbuf_ring("grouped_qk", b, 2, [P, QK_COLS, PACK], BF16)
             for side in range(SIDES):
                 side_cols = slice(side * SIDE_COLS, (side + 1) * SIDE_COLS)
-                nc.gpsimd.tensor_scalar(
-                    out=grouped[:, side_cols, :],
-                    in0=normed[:, :, side_cols].rearrange("p t c -> p c t"),
-                    scalar1=1.0,
-                    scalar2=0.0,
-                    op0=ALU.mult,
-                    op1=ALU.add,
+                nc.vector.tensor_copy(
+                    out=grouped[:, side_cols, :].rearrange("p (c i) t -> p c t i", i=4),
+                    in_=normed[:, :, side_cols].rearrange("p t (c i) -> p c t i", i=4),
                 )
             return grouped
 
@@ -164,7 +162,7 @@ def tile_transposedattentiontransformer_pa_t_kernel(tc, h, w_qk, w_q_norm, w_k_n
             )
 
         def scores(b):
-            att = sums_pool.tile([P, HEADS, HEAD_DIM], F32, tag="sums")
+            att = psum_ring("sums", SIDES * TOKEN_TILES * BATCH + b, SUM_BANKS, [P, HEADS, HEAD_DIM])
             for g in range(HEADS):
                 q_cols = slice(g * HEAD_DIM, (g + 1) * HEAD_DIM)
                 k_cols = slice(SIDE_COLS + g * HEAD_DIM, SIDE_COLS + (g + 1) * HEAD_DIM)
@@ -177,15 +175,15 @@ def tile_transposedattentiontransformer_pa_t_kernel(tc, h, w_qk, w_q_norm, w_k_n
                     start=True,
                     stop=True,
                 )
-            top = small.tile([P, HEADS], F32, tag="top")
+            top = sbuf_ring("top", b, 3, [P, HEADS], F32)
             nc.vector.tensor_reduce(out=top[:], in_=att[:], axis=mybir.AxisListType.X, op=ALU.max)
-            shift = small.tile([P, HEADS], F32, tag="shift")
+            shift = sbuf_ring("shift", b, 3, [P, HEADS], F32)
             nc.vector.tensor_scalar_mul(out=shift[:], in0=top[:], scalar1=-SOFTMAX_SCALE)
             return att, shift
 
-        def exponentials(att, shift):
-            weights = soft.tile([P, HEADS, HEAD_DIM], F32, tag="weights")
-            total = small.tile([P, HEADS], F32, tag="total")
+        def exponentials(att, shift, b):
+            weights = sbuf_ring("weights", b, 3, [P, HEADS, HEAD_DIM], F32)
+            total = sbuf_ring("total", b, 3, [P, HEADS], F32)
             for g in range(HEADS):
                 nc.scalar.activation(
                     out=weights[:, g, :],
@@ -198,7 +196,7 @@ def tile_transposedattentiontransformer_pa_t_kernel(tc, h, w_qk, w_q_norm, w_k_n
             return weights, total
 
         def divide_and_store(weights, total, b):
-            inv_total = small.tile([P, HEADS], F32, tag="inv_total")
+            inv_total = sbuf_ring("inv_total", b, 3, [P, HEADS], F32)
             nc.vector.reciprocal(out=inv_total[:], in_=total[:])
             for g in range(HEADS):
                 nc.vector.tensor_scalar_mul(out=weights[:, g, :], in0=weights[:, g, :], scalar1=inv_total[:, g : g + 1])
@@ -208,30 +206,32 @@ def tile_transposedattentiontransformer_pa_t_kernel(tc, h, w_qk, w_q_norm, w_k_n
         weight_rows = [load_weight_rows(side) for side in range(SIDES)]
         token_rows[1] = load_token_rows(1)
 
-        token_codes = {0: new_token_codes()}
-        quantise_rows(gather_words(transpose_rows(token_rows[0])), token_codes[0][0][:], token_codes[0][1][:])
+        token_codes = {0: new_token_codes(0)}
+        quantise_rows(gather_words(transpose_rows(token_rows[0]), 0), token_codes[0][0][:], token_codes[0][1][:])
         for side in range(SIDES):
             side_cols = slice(side * SIDE_COLS, (side + 1) * SIDE_COLS)
-            quantise_rows(gather_words(transpose_rows(weight_rows[side])), w_codes[:, side_cols], w_scales[:, side_cols])
+            grouped_rows = gather_words(transpose_rows(weight_rows[side]), 1 + side)
+            quantise_rows(grouped_rows, w_codes[:, side_cols], w_scales[:, side_cols])
 
         grouped_qk = {}
         for b in range(BATCH):
             if b + 2 < BATCH:
                 token_rows[b + 2] = load_token_rows(b + 2)
             h_codes, h_scales = token_codes[b]
-            normed = stage.tile([P, TOKEN_TILES, QK_COLS], BF16, tag="normed")
+            normed = sbuf_ring("normed", b, 2, [P, TOKEN_TILES, QK_COLS], BF16)
             for t in range(TOKEN_TILES):
-                raw = project(h_codes, h_scales, t)
-                rms = measure(raw)
+                step = TOKEN_TILES * b + t
+                raw = project(h_codes, h_scales, t, step)
+                rms = measure(raw, step)
                 if b + 1 < BATCH and t == 0:
                     banks = transpose_rows(token_rows[b + 1])
                 if b + 1 < BATCH and t == 1:
-                    grouped_rows = gather_words(banks)
-                normalise(raw, rms, normed[:, t, :])
+                    grouped_rows = gather_words(banks, b + 1)
+                normalise(raw, rms, normed[:, t, :], step)
                 if b + 1 < BATCH and t == 2:
-                    token_codes[b + 1] = new_token_codes()
+                    token_codes[b + 1] = new_token_codes(b + 1)
                     quantise_rows(grouped_rows, token_codes[b + 1][0][:], token_codes[b + 1][1][:])
-            grouped_qk[b] = regroup(normed)
+            grouped_qk[b] = regroup(normed, b)
             if b > 0:
                 quantise_qk(grouped_qk[b - 1], b - 1)
 
@@ -242,5 +242,5 @@ def tile_transposedattentiontransformer_pa_t_kernel(tc, h, w_qk, w_q_norm, w_k_n
             if b + 1 < BATCH:
                 waiting[b + 1] = scores(b + 1)
             att, shift = waiting[b]
-            weights, total = exponentials(att, shift)
+            weights, total = exponentials(att, shift, b)
             divide_and_store(weights, total, b)

@@ -52,7 +52,6 @@ def tile_transposedattentiontransformer_pa_t_kernel(tc, h, w_qk, w_q_norm, w_k_n
         gains = const.tile([P, SIDES, HEAD_DIM], BF16)
         nc.scalar.dma_start(out=gains[:, 0, :], in_=w_q_norm.partition_broadcast(P))
         nc.scalar.dma_start(out=gains[:, 1, :], in_=w_k_norm.partition_broadcast(P))
-        squares = const.tile([P, HEAD_DIM], BF16)
 
         w_codes = const.tile([P, QK_COLS], U32, align_bytes=64)
         w_scales = const.tile([P, QK_COLS], U8, align_bytes=64)
@@ -86,8 +85,8 @@ def tile_transposedattentiontransformer_pa_t_kernel(tc, h, w_qk, w_q_norm, w_k_n
         def gather_words(banks, call):
             grouped = sbuf_ring("grouped_rows", call, 2, [P, ROW_TILES * P * PACK], BF16)
             pairs = grouped[:].bitcast(F32).rearrange("p (n r k u) -> p n r k u", n=2, r=2, u=2)
-            nc.scalar.copy(out=pairs[:, 0], in_=banks[0][:].rearrange("p (r u) k -> p r k u", u=2))
-            nc.vector.tensor_copy(out=pairs[:, 1], in_=banks[1][:].rearrange("p (r u) k -> p r k u", u=2))
+            for n in range(2):
+                nc.scalar.copy(out=pairs[:, n], in_=banks[n][:].rearrange("p (r u) k -> p r k u", u=2))
             return grouped
 
         def quantise_rows(grouped, codes, scales):
@@ -116,16 +115,20 @@ def tile_transposedattentiontransformer_pa_t_kernel(tc, h, w_qk, w_q_norm, w_k_n
                 raw.append(sums)
             return raw
 
-        def measure(raw, step):
-            sumsq = sbuf_ring("sumsq", step, 4, [P, SIDES * HEADS], F32)
+        def square(raw, step):
+            squares = sbuf_ring("squares", step, 3, [P, SIDES, SIDE_COLS], F32)
             for side in range(SIDES):
-                for g in range(HEADS):
-                    nc.scalar.activation(
-                        out=squares[:],
-                        in_=raw[side][:, g * HEAD_DIM : (g + 1) * HEAD_DIM],
-                        func=ACT.Square,
-                        accum_out=sumsq[:, side * HEADS + g : side * HEADS + g + 1],
-                    )
+                nc.scalar.activation(out=squares[:, side, :], in_=raw[side][:], func=ACT.Square)
+            return squares
+
+        def root_mean(squares, step):
+            sumsq = sbuf_ring("sumsq", step, 4, [P, SIDES * HEADS], F32)
+            nc.vector.tensor_reduce(
+                out=sumsq[:],
+                in_=squares[:].rearrange("p s (g d) -> p (s g) d", d=HEAD_DIM),
+                axis=mybir.AxisListType.X,
+                op=ALU.add,
+            )
             rms = sbuf_ring("rms", step, 4, [P, SIDES * HEADS], F32)
             nc.scalar.activation(out=rms[:], in_=sumsq[:], func=ACT.Sqrt, scale=1.0 / HEAD_DIM, bias=eps[:])
             return rms
@@ -148,9 +151,13 @@ def tile_transposedattentiontransformer_pa_t_kernel(tc, h, w_qk, w_q_norm, w_k_n
             grouped = sbuf_ring("grouped_qk", b, 2, [P, QK_COLS, PACK], BF16)
             for side in range(SIDES):
                 side_cols = slice(side * SIDE_COLS, (side + 1) * SIDE_COLS)
-                nc.vector.tensor_copy(
-                    out=grouped[:, side_cols, :].rearrange("p (c i) t -> p c t i", i=4),
-                    in_=normed[:, :, side_cols].rearrange("p t (c i) -> p c t i", i=4),
+                nc.gpsimd.tensor_scalar(
+                    out=grouped[:, side_cols, :],
+                    in0=normed[:, :, side_cols].rearrange("p t c -> p c t"),
+                    scalar1=1.0,
+                    scalar2=0.0,
+                    op0=ALU.mult,
+                    op1=ALU.add,
                 )
             return grouped
 
@@ -213,27 +220,33 @@ def tile_transposedattentiontransformer_pa_t_kernel(tc, h, w_qk, w_q_norm, w_k_n
             grouped_rows = gather_words(transpose_rows(weight_rows[side]), 1 + side)
             quantise_rows(grouped_rows, w_codes[:, side_cols], w_scales[:, side_cols])
 
-        grouped_qk = {}
-        for b in range(BATCH):
-            if b + 2 < BATCH:
-                token_rows[b + 2] = load_token_rows(b + 2)
-            h_codes, h_scales = token_codes[b]
-            normed = sbuf_ring("normed", b, 2, [P, TOKEN_TILES, QK_COLS], BF16)
-            for t in range(TOKEN_TILES):
-                step = TOKEN_TILES * b + t
-                raw = project(h_codes, h_scales, t, step)
-                rms = measure(raw, step)
+        steps = BATCH * TOKEN_TILES
+        raw, squares, rms, normed, grouped_qk = {}, {}, {}, {}, {}
+        for s in range(steps + 2):
+            if s < steps:
+                b, t = divmod(s, TOKEN_TILES)
+                raw[s] = project(token_codes[b][0], token_codes[b][1], t, s)
+                squares[s] = square(raw[s], s)
                 if b + 1 < BATCH and t == 0:
                     banks = transpose_rows(token_rows[b + 1])
+                    if b + 2 < BATCH:
+                        token_rows[b + 2] = load_token_rows(b + 2)
                 if b + 1 < BATCH and t == 1:
                     grouped_rows = gather_words(banks, b + 1)
-                normalise(raw, rms, normed[:, t, :], step)
-                if b + 1 < BATCH and t == 2:
-                    token_codes[b + 1] = new_token_codes(b + 1)
-                    quantise_rows(grouped_rows, token_codes[b + 1][0][:], token_codes[b + 1][1][:])
-            grouped_qk[b] = regroup(normed, b)
-            if b > 0:
-                quantise_qk(grouped_qk[b - 1], b - 1)
+            if 1 <= s <= steps:
+                rms[s - 1] = root_mean(squares[s - 1], s - 1)
+            if s < steps and b + 1 < BATCH and t == 2:
+                token_codes[b + 1] = new_token_codes(b + 1)
+                quantise_rows(grouped_rows, token_codes[b + 1][0][:], token_codes[b + 1][1][:])
+            if s >= 2:
+                done_b, done_t = divmod(s - 2, TOKEN_TILES)
+                if done_t == 0:
+                    normed[done_b] = sbuf_ring("normed", done_b, 2, [P, TOKEN_TILES, QK_COLS], BF16)
+                normalise(raw[s - 2], rms[s - 2], normed[done_b][:, done_t, :], s - 2)
+                if done_t == TOKEN_TILES - 1:
+                    grouped_qk[done_b] = regroup(normed[done_b], done_b)
+                    if done_b > 0:
+                        quantise_qk(grouped_qk[done_b - 1], done_b - 1)
 
         waiting = {0: scores(0)}
         for b in range(BATCH):

@@ -26,6 +26,7 @@ ROW_TILES = 4
 TOKEN_TILES = TOKENS // P
 SIDE_COLS = HEADS * HEAD_DIM
 QK_COLS = SIDES * SIDE_COLS
+GROUPS = SIDES * HEADS
 SUM_BANKS = 6
 
 FLOPS = 2 * BATCH * TOKENS * CHANNELS * QK_COLS + 2 * BATCH * HEADS * HEAD_DIM * HEAD_DIM * TOKENS
@@ -97,69 +98,50 @@ def tile_transposedattentiontransformer_pa_t_kernel(tc, h, w_qk, w_q_norm, w_k_n
             h_scales = sbuf_ring("h_scales", b, 2, [P, TOKENS], U8)
             return h_codes, h_scales
 
-        def project(h_codes, h_scales, t, step):
-            token_cols = slice(t * P, (t + 1) * P)
-            raw = []
-            for side in range(SIDES):
-                side_cols = slice(side * SIDE_COLS, (side + 1) * SIDE_COLS)
-                sums = psum_ring("sums", SIDES * step + side, SUM_BANKS, [P, SIDE_COLS])
+        def project(h_codes, h_scales, group, unit):
+            group_cols = slice(group * HEAD_DIM, (group + 1) * HEAD_DIM)
+            sums = psum_ring("sums", unit, SUM_BANKS, [P, TOKEN_TILES, HEAD_DIM])
+            for t in range(TOKEN_TILES):
+                token_cols = slice(t * P, (t + 1) * P)
                 nc.tensor.matmul_mx(
-                    out=sums[:],
+                    out=sums[:, t, :],
                     lhsT=h_codes[:, token_cols].bitcast(FP8X4),
                     lhsT_scale=h_scales[:, token_cols],
-                    rhs=w_codes[:, side_cols].bitcast(FP8X4),
-                    rhs_scale=w_scales[:, side_cols],
+                    rhs=w_codes[:, group_cols].bitcast(FP8X4),
+                    rhs_scale=w_scales[:, group_cols],
                     start=True,
                     stop=True,
                 )
-                raw.append(sums)
-            return raw
+            return sums
 
-        def square(raw, step):
-            squares = sbuf_ring("squares", step, 3, [P, SIDES, SIDE_COLS], F32)
-            for side in range(SIDES):
-                nc.scalar.activation(out=squares[:, side, :], in_=raw[side][:], func=ACT.Square)
+        def square(sums, unit):
+            squares = sbuf_ring("squares", unit, 3, [P, TOKEN_TILES, HEAD_DIM], F32)
+            nc.scalar.activation(out=squares[:], in_=sums[:], func=ACT.Square)
             return squares
 
-        def root_mean(squares, step):
-            sumsq = sbuf_ring("sumsq", step, 4, [P, SIDES * HEADS], F32)
-            nc.vector.tensor_reduce(
-                out=sumsq[:],
-                in_=squares[:].rearrange("p s (g d) -> p (s g) d", d=HEAD_DIM),
-                axis=mybir.AxisListType.X,
-                op=ALU.add,
+        def inverse_rms(squares, unit):
+            sumsq = sbuf_ring("sumsq", unit, 4, [P, TOKEN_TILES], F32)
+            nc.vector.tensor_reduce(out=sumsq[:], in_=squares[:], axis=mybir.AxisListType.X, op=ALU.add)
+            inv_rms = sbuf_ring("inv_rms", unit, 4, [P, TOKEN_TILES], F32)
+            nc.scalar.activation(
+                out=inv_rms[:], in_=sumsq[:], func=ACT.Abs_reciprocal_sqrt, scale=1.0 / HEAD_DIM, bias=eps[:]
             )
-            rms = sbuf_ring("rms", step, 4, [P, SIDES * HEADS], F32)
-            nc.scalar.activation(out=rms[:], in_=sumsq[:], func=ACT.Sqrt, scale=1.0 / HEAD_DIM, bias=eps[:])
-            return rms
+            return inv_rms
 
-        def normalise(raw, rms, normed_rows, step):
-            inv_rms = sbuf_ring("inv_rms", step, 4, [P, SIDES * HEADS], F32)
-            nc.vector.reciprocal(out=inv_rms[:], in_=rms[:])
-            for side in range(SIDES):
-                for g in range(HEADS):
-                    nc.vector.scalar_tensor_tensor(
-                        out=normed_rows[:, side * SIDE_COLS + g * HEAD_DIM : side * SIDE_COLS + (g + 1) * HEAD_DIM],
-                        in0=raw[side][:, g * HEAD_DIM : (g + 1) * HEAD_DIM],
-                        scalar=inv_rms[:, side * HEADS + g : side * HEADS + g + 1],
-                        in1=gains[:, side, :],
-                        op0=ALU.mult,
-                        op1=ALU.mult,
-                    )
+        def factor_table(inv_rms, side, unit):
+            factors = sbuf_ring("factors", unit, 3, [P, HEAD_DIM, PACK], F32)
+            nc.gpsimd.tensor_tensor(
+                out=factors[:],
+                in0=gains[:, side, :].unsqueeze(2).to_broadcast([P, HEAD_DIM, PACK]),
+                in1=inv_rms[:].unsqueeze(1).to_broadcast([P, HEAD_DIM, PACK]),
+                op=ALU.mult,
+            )
+            return factors
 
-        def regroup(normed, b):
-            grouped = sbuf_ring("grouped_qk", b, 2, [P, QK_COLS, PACK], BF16)
-            for side in range(SIDES):
-                side_cols = slice(side * SIDE_COLS, (side + 1) * SIDE_COLS)
-                nc.gpsimd.tensor_scalar(
-                    out=grouped[:, side_cols, :],
-                    in0=normed[:, :, side_cols].rearrange("p t c -> p c t"),
-                    scalar1=1.0,
-                    scalar2=0.0,
-                    op0=ALU.mult,
-                    op1=ALU.add,
-                )
-            return grouped
+        def normalise(sums, factors, grouped_cols):
+            nc.vector.tensor_tensor(
+                out=grouped_cols, in0=sums[:].rearrange("p t c -> p c t"), in1=factors[:], op=ALU.mult
+            )
 
         def quantise_qk(grouped, b):
             nc.vector.quantize_mx(
@@ -169,7 +151,7 @@ def tile_transposedattentiontransformer_pa_t_kernel(tc, h, w_qk, w_q_norm, w_k_n
             )
 
         def scores(b):
-            att = psum_ring("sums", SIDES * TOKEN_TILES * BATCH + b, SUM_BANKS, [P, HEADS, HEAD_DIM])
+            att = psum_ring("sums", GROUPS * BATCH + b, SUM_BANKS, [P, HEADS, HEAD_DIM])
             for g in range(HEADS):
                 q_cols = slice(g * HEAD_DIM, (g + 1) * HEAD_DIM)
                 k_cols = slice(SIDE_COLS + g * HEAD_DIM, SIDE_COLS + (g + 1) * HEAD_DIM)
@@ -220,33 +202,32 @@ def tile_transposedattentiontransformer_pa_t_kernel(tc, h, w_qk, w_q_norm, w_k_n
             grouped_rows = gather_words(transpose_rows(weight_rows[side]), 1 + side)
             quantise_rows(grouped_rows, w_codes[:, side_cols], w_scales[:, side_cols])
 
-        steps = BATCH * TOKEN_TILES
-        raw, squares, rms, normed, grouped_qk = {}, {}, {}, {}, {}
-        for s in range(steps + 2):
-            if s < steps:
-                b, t = divmod(s, TOKEN_TILES)
-                raw[s] = project(token_codes[b][0], token_codes[b][1], t, s)
-                squares[s] = square(raw[s], s)
-                if b + 1 < BATCH and t == 0:
+        units = BATCH * GROUPS
+        sums, squares, factors, grouped_qk = {}, {}, {}, {}
+        for u in range(units + 3):
+            if u < units:
+                b, group = divmod(u, GROUPS)
+                sums[u] = project(token_codes[b][0], token_codes[b][1], group, u)
+                squares[u] = square(sums[u], u)
+                if b + 1 < BATCH and group == 0:
                     banks = transpose_rows(token_rows[b + 1])
                     if b + 2 < BATCH:
                         token_rows[b + 2] = load_token_rows(b + 2)
-                if b + 1 < BATCH and t == 1:
+                if b + 1 < BATCH and group == 2:
                     grouped_rows = gather_words(banks, b + 1)
-            if 1 <= s <= steps:
-                rms[s - 1] = root_mean(squares[s - 1], s - 1)
-            if s < steps and b + 1 < BATCH and t == 2:
+            if 1 <= u <= units:
+                factors[u - 1] = factor_table(inverse_rms(squares[u - 1], u - 1), ((u - 1) % GROUPS) // HEADS, u - 1)
+            if u < units and b + 1 < BATCH and group == 4:
                 token_codes[b + 1] = new_token_codes(b + 1)
                 quantise_rows(grouped_rows, token_codes[b + 1][0][:], token_codes[b + 1][1][:])
-            if s >= 2:
-                done_b, done_t = divmod(s - 2, TOKEN_TILES)
-                if done_t == 0:
-                    normed[done_b] = sbuf_ring("normed", done_b, 2, [P, TOKEN_TILES, QK_COLS], BF16)
-                normalise(raw[s - 2], rms[s - 2], normed[done_b][:, done_t, :], s - 2)
-                if done_t == TOKEN_TILES - 1:
-                    grouped_qk[done_b] = regroup(normed[done_b], done_b)
-                    if done_b > 0:
-                        quantise_qk(grouped_qk[done_b - 1], done_b - 1)
+            if u >= 3:
+                done_b, done_group = divmod(u - 3, GROUPS)
+                if done_group == 0:
+                    grouped_qk[done_b] = sbuf_ring("grouped_qk", done_b, 2, [P, QK_COLS, PACK], BF16)
+                done_cols = slice(done_group * HEAD_DIM, (done_group + 1) * HEAD_DIM)
+                normalise(sums[u - 3], factors[u - 3], grouped_qk[done_b][:, done_cols, :])
+                if done_group == 0 and done_b > 0:
+                    quantise_qk(grouped_qk[done_b - 1], done_b - 1)
 
         waiting = {0: scores(0)}
         for b in range(BATCH):

@@ -114,39 +114,54 @@ def tile_transposedattentiontransformer_pa_t_kernel(tc, h, w_qk, w_q_norm, w_k_n
                 )
             return sums
 
-        def square(sums, unit):
-            squares = sbuf_ring("squares", unit, 3, [P, TOKEN_TILES, HEAD_DIM], F32)
-            nc.scalar.activation(out=squares[:], in_=sums[:], func=ACT.Square)
-            return squares
+        def sum_squares(sums, unit, sumsq):
+            squares = sbuf_ring("squares", unit, 4, [P, TOKEN_TILES, HEAD_DIM], F32)
+            for t in range(TOKEN_TILES):
+                nc.scalar.activation(
+                    out=squares[:, t, :],
+                    in_=sums[:, t, :],
+                    func=ACT.Square,
+                    accum_out=sumsq[:, unit % 2, t : t + 1],
+                )
 
-        def inverse_rms(squares, unit):
-            sumsq = sbuf_ring("sumsq", unit, 4, [P, TOKEN_TILES], F32)
-            nc.vector.tensor_reduce(out=sumsq[:], in_=squares[:], axis=mybir.AxisListType.X, op=ALU.add)
-            inv_rms = sbuf_ring("inv_rms", unit, 4, [P, TOKEN_TILES], F32)
+        def inverse_rms(sumsq, pair):
+            inv_rms = sbuf_ring("inv_rms", pair, 4, [P, 2, TOKEN_TILES], F32)
             nc.scalar.activation(
                 out=inv_rms[:], in_=sumsq[:], func=ACT.Abs_reciprocal_sqrt, scale=1.0 / HEAD_DIM, bias=eps[:]
             )
             return inv_rms
 
-        def factor_table(inv_rms, side, unit):
-            factors = sbuf_ring("factors", unit, 3, [P, HEAD_DIM, PACK], F32)
-            nc.gpsimd.tensor_tensor(
-                out=factors[:],
-                in0=gains[:, side, :].unsqueeze(2).to_broadcast([P, HEAD_DIM, PACK]),
-                in1=inv_rms[:].unsqueeze(1).to_broadcast([P, HEAD_DIM, PACK]),
-                op=ALU.mult,
-            )
-            return factors
+        def normalise(sums, inv_rms, unit, rows):
+            side = (unit % GROUPS) // HEADS
+            head_cols = slice((unit % HEADS) * HEAD_DIM, (unit % HEADS + 1) * HEAD_DIM)
+            for t in range(TOKEN_TILES):
+                nc.vector.scalar_tensor_tensor(
+                    out=rows[:, t, head_cols],
+                    in0=sums[:, t, :],
+                    scalar=inv_rms[:, unit % 2, t : t + 1],
+                    in1=gains[:, side, :],
+                    op0=ALU.mult,
+                    op1=ALU.mult,
+                )
 
-        def normalise(sums, factors, grouped_cols):
-            nc.vector.tensor_tensor(
-                out=grouped_cols, in0=sums[:].rearrange("p t c -> p c t"), in1=factors[:], op=ALU.mult
+        def interleave(rows, index):
+            grouped = sbuf_ring("grouped_qk", index, 3, [P, SIDE_COLS, PACK], BF16)
+            nc.gpsimd.tensor_scalar(
+                out=grouped[:],
+                in0=rows[:].rearrange("p t c -> p c t"),
+                scalar1=1.0,
+                scalar2=0.0,
+                op0=ALU.mult,
+                op1=ALU.add,
             )
+            return grouped
 
-        def quantise_qk(grouped, b):
+        def quantise_qk(grouped, index):
+            b, side = divmod(index, SIDES)
+            cols = slice(side * SIDE_COLS, (side + 1) * SIDE_COLS)
             nc.vector.quantize_mx(
-                out=qk_codes[:, b, :].bitcast(FP8X4),
-                scales=qk_scales[:, b, :],
+                out=qk_codes[:, b, cols].bitcast(FP8X4),
+                scales=qk_scales[:, b, cols],
                 in_=grouped[:].rearrange("p c t -> p (c t)"),
             )
 
@@ -202,37 +217,42 @@ def tile_transposedattentiontransformer_pa_t_kernel(tc, h, w_qk, w_q_norm, w_k_n
             grouped_rows = gather_words(transpose_rows(weight_rows[side]), 1 + side)
             quantise_rows(grouped_rows, w_codes[:, side_cols], w_scales[:, side_cols])
 
-        units = BATCH * GROUPS
-        sums, squares, factors, grouped_qk = {}, {}, {}, {}
-        for u in range(units + 3):
-            if u < units:
-                b, group = divmod(u, GROUPS)
-                sums[u] = project(token_codes[b][0], token_codes[b][1], group, u)
-                squares[u] = square(sums[u], u)
-                if b + 1 < BATCH and group == 0:
+        pairs = BATCH * GROUPS // 2
+        sums, sumsq, inv_rms, rows, grouped_qk = {}, {}, {}, {}, {}
+        for s in range(pairs + 3):
+            b, step = divmod(s, GROUPS // 2)
+            if s < pairs:
+                sumsq[s] = sbuf_ring("sumsq", s, 4, [P, 2, TOKEN_TILES], F32)
+            for i in range(2):
+                if s < pairs:
+                    unit = 2 * s + i
+                    sums[unit] = project(token_codes[b][0], token_codes[b][1], unit % GROUPS, unit)
+                    sum_squares(sums[unit], unit, sumsq[s])
+                if i == 0 and 1 <= s <= pairs:
+                    inv_rms[s - 1] = inverse_rms(sumsq[s - 1], s - 1)
+            if s < pairs and b + 1 < BATCH:
+                if step == 0:
                     banks = transpose_rows(token_rows[b + 1])
                     if b + 2 < BATCH:
                         token_rows[b + 2] = load_token_rows(b + 2)
-                if b + 1 < BATCH and group == 2:
+                if step == 1:
                     grouped_rows = gather_words(banks, b + 1)
-            if 1 <= u <= units:
-                factors[u - 1] = factor_table(inverse_rms(squares[u - 1], u - 1), ((u - 1) % GROUPS) // HEADS, u - 1)
-            if u < units and b + 1 < BATCH and group == 4:
-                token_codes[b + 1] = new_token_codes(b + 1)
-                quantise_rows(grouped_rows, token_codes[b + 1][0][:], token_codes[b + 1][1][:])
-            if u >= 3:
-                done_b, done_group = divmod(u - 3, GROUPS)
-                if done_group == 0:
-                    grouped_qk[done_b] = sbuf_ring("grouped_qk", done_b, 2, [P, QK_COLS, PACK], BF16)
-                done_cols = slice(done_group * HEAD_DIM, (done_group + 1) * HEAD_DIM)
-                normalise(sums[u - 3], factors[u - 3], grouped_qk[done_b][:, done_cols, :])
-                if done_group == 0 and done_b > 0:
-                    quantise_qk(grouped_qk[done_b - 1], done_b - 1)
+                if step == 2:
+                    token_codes[b + 1] = new_token_codes(b + 1)
+                    quantise_rows(grouped_rows, token_codes[b + 1][0][:], token_codes[b + 1][1][:])
+            if 1 <= s <= pairs:
+                index, half = divmod(s - 1, 2)
+                if half == 0:
+                    rows[index] = sbuf_ring("rows_qk", index, 3, [P, TOKEN_TILES, SIDE_COLS], BF16)
+                for unit in (2 * s - 2, 2 * s - 1):
+                    normalise(sums[unit], inv_rms[s - 1], unit, rows[index])
+                if half == 1:
+                    grouped_qk[index] = interleave(rows[index], index)
+            if s >= 4 and s % 2 == 0:
+                quantise_qk(grouped_qk[s // 2 - 2], s // 2 - 2)
 
         waiting = {0: scores(0)}
         for b in range(BATCH):
-            if b + 1 == BATCH - 1:
-                quantise_qk(grouped_qk[b + 1], b + 1)
             if b + 1 < BATCH:
                 waiting[b + 1] = scores(b + 1)
             att, shift = waiting[b]

@@ -144,17 +144,16 @@ def tile_transposedattentiontransformer_pa_t_kernel(tc, h, w_qk, w_q_norm, w_k_n
                     op1=ALU.mult,
                 )
 
-        def interleave(rows, index):
-            grouped = sbuf_ring("grouped_qk", index, 3, [P, SIDE_COLS, PACK], BF16)
+        def interleave(rows, grouped, unit):
+            head_cols = slice((unit % HEADS) * HEAD_DIM, (unit % HEADS + 1) * HEAD_DIM)
             nc.gpsimd.tensor_scalar(
-                out=grouped[:],
-                in0=rows[:].rearrange("p t c -> p c t"),
+                out=grouped[:, head_cols, :],
+                in0=rows[:, :, head_cols].rearrange("p t c -> p c t"),
                 scalar1=1.0,
                 scalar2=0.0,
                 op0=ALU.mult,
                 op1=ALU.add,
             )
-            return grouped
 
         def quantise_qk(grouped, index):
             b, side = divmod(index, SIDES)
@@ -244,10 +243,10 @@ def tile_transposedattentiontransformer_pa_t_kernel(tc, h, w_qk, w_q_norm, w_k_n
                 index, half = divmod(s - 1, 2)
                 if half == 0:
                     rows[index] = sbuf_ring("rows_qk", index, 3, [P, TOKEN_TILES, SIDE_COLS], BF16)
+                    grouped_qk[index] = sbuf_ring("grouped_qk", index, 3, [P, SIDE_COLS, PACK], BF16)
                 for unit in (2 * s - 2, 2 * s - 1):
                     normalise(sums[unit], inv_rms[s - 1], unit, rows[index])
-                if half == 1:
-                    grouped_qk[index] = interleave(rows[index], index)
+                    interleave(rows[index], grouped_qk[index], unit)
             if s >= 4 and s % 2 == 0:
                 quantise_qk(grouped_qk[s // 2 - 2], s // 2 - 2)
 

@@ -51,8 +51,8 @@ def tile_transposedattentiontransformer_pa_t_kernel(tc, h, w_qk, w_q_norm, w_k_n
         eps = const.tile([P, 1], F32)
         nc.vector.memset(eps[:], EPS)
         gains = const.tile([P, SIDES, HEAD_DIM], BF16)
-        nc.scalar.dma_start(out=gains[:, 0, :], in_=w_q_norm.partition_broadcast(P))
-        nc.scalar.dma_start(out=gains[:, 1, :], in_=w_k_norm.partition_broadcast(P))
+        first_root = const.tile([P, 1], F32)
+        nc.scalar.activation(out=first_root[:], in_=eps[:], func=ACT.Abs_reciprocal_sqrt)
 
         w_codes = const.tile([P, QK_COLS], U32, align_bytes=64)
         w_scales = const.tile([P, QK_COLS], U8, align_bytes=64)
@@ -83,11 +83,11 @@ def tile_transposedattentiontransformer_pa_t_kernel(tc, h, w_qk, w_q_norm, w_k_n
                 banks.append(turned)
             return banks
 
-        def gather_words(banks, call):
+        def gather_words(banks, call, second_copy):
             grouped = sbuf_ring("grouped_rows", call, 2, [P, ROW_TILES * P * PACK], BF16)
             pairs = grouped[:].bitcast(F32).rearrange("p (n r k u) -> p n r k u", n=2, r=2, u=2)
-            for n in range(2):
-                nc.scalar.copy(out=pairs[:, n], in_=banks[n][:].rearrange("p (r u) k -> p r k u", u=2))
+            for n, copy in enumerate((nc.scalar.copy, second_copy)):
+                copy(out=pairs[:, n], in_=banks[n][:].rearrange("p (r u) k -> p r k u", u=2))
             return grouped
 
         def quantise_rows(grouped, codes, scales):
@@ -133,7 +133,7 @@ def tile_transposedattentiontransformer_pa_t_kernel(tc, h, w_qk, w_q_norm, w_k_n
 
         def normalise(sums, inv_rms, unit, rows):
             side = (unit % GROUPS) // HEADS
-            head_cols = slice((unit % HEADS) * HEAD_DIM, (unit % HEADS + 1) * HEAD_DIM)
+            head_cols = slice((unit % GROUPS) * HEAD_DIM, (unit % GROUPS + 1) * HEAD_DIM)
             for t in range(TOKEN_TILES):
                 nc.vector.scalar_tensor_tensor(
                     out=rows[:, t, head_cols],
@@ -145,7 +145,7 @@ def tile_transposedattentiontransformer_pa_t_kernel(tc, h, w_qk, w_q_norm, w_k_n
                 )
 
         def interleave(rows, grouped, unit):
-            head_cols = slice((unit % HEADS) * HEAD_DIM, (unit % HEADS + 1) * HEAD_DIM)
+            head_cols = slice((unit % GROUPS) * HEAD_DIM, (unit % GROUPS + 1) * HEAD_DIM)
             nc.gpsimd.tensor_scalar(
                 out=grouped[:, head_cols, :],
                 in0=rows[:, :, head_cols].rearrange("p t c -> p c t"),
@@ -155,12 +155,10 @@ def tile_transposedattentiontransformer_pa_t_kernel(tc, h, w_qk, w_q_norm, w_k_n
                 op1=ALU.add,
             )
 
-        def quantise_qk(grouped, index):
-            b, side = divmod(index, SIDES)
-            cols = slice(side * SIDE_COLS, (side + 1) * SIDE_COLS)
+        def quantise_qk(grouped, b):
             nc.vector.quantize_mx(
-                out=qk_codes[:, b, cols].bitcast(FP8X4),
-                scales=qk_scales[:, b, cols],
+                out=qk_codes[:, b, :].bitcast(FP8X4),
+                scales=qk_scales[:, b, :],
                 in_=grouped[:].rearrange("p c t -> p (c t)"),
             )
 
@@ -178,15 +176,17 @@ def tile_transposedattentiontransformer_pa_t_kernel(tc, h, w_qk, w_q_norm, w_k_n
                     start=True,
                     stop=True,
                 )
-            top = sbuf_ring("top", b, 3, [P, HEADS], F32)
+            top = sbuf_ring("top", b, 4, [P, HEADS], F32)
             nc.vector.tensor_reduce(out=top[:], in_=att[:], axis=mybir.AxisListType.X, op=ALU.max)
-            shift = sbuf_ring("shift", b, 3, [P, HEADS], F32)
-            nc.vector.tensor_scalar_mul(out=shift[:], in0=top[:], scalar1=-SOFTMAX_SCALE)
+            shift = sbuf_ring("shift", b, 4, [P, HEADS], F32)
+            nc.gpsimd.tensor_scalar(
+                out=shift[:], in0=top[:], scalar1=-SOFTMAX_SCALE, scalar2=0.0, op0=ALU.mult, op1=ALU.add
+            )
             return att, shift
 
         def exponentials(att, shift, b):
-            weights = sbuf_ring("weights", b, 3, [P, HEADS, HEAD_DIM], F32)
-            total = sbuf_ring("total", b, 3, [P, HEADS], F32)
+            weights = sbuf_ring("weights", b, 4, [P, HEADS, HEAD_DIM], F32)
+            total = sbuf_ring("total", b, 4, [P, HEADS], F32)
             for g in range(HEADS):
                 nc.scalar.activation(
                     out=weights[:, g, :],
@@ -199,27 +199,39 @@ def tile_transposedattentiontransformer_pa_t_kernel(tc, h, w_qk, w_q_norm, w_k_n
             return weights, total
 
         def divide_and_store(weights, total, b):
-            inv_total = sbuf_ring("inv_total", b, 3, [P, HEADS], F32)
+            inv_total = sbuf_ring("inv_total", b, 4, [P, HEADS], F32)
             nc.vector.reciprocal(out=inv_total[:], in_=total[:])
             for g in range(HEADS):
-                nc.vector.tensor_scalar_mul(out=weights[:, g, :], in0=weights[:, g, :], scalar1=inv_total[:, g : g + 1])
+                engine = nc.vector if g < HEADS // 2 else nc.gpsimd
+                engine.tensor_scalar(
+                    out=weights[:, g, :],
+                    in0=weights[:, g, :],
+                    scalar1=inv_total[:, g : g + 1],
+                    scalar2=0.0,
+                    op0=ALU.mult,
+                    op1=ALU.add,
+                )
             nc.sync.dma_start(out=out[b].rearrange("g d e -> d g e"), in_=weights[:])
 
         token_rows = {0: load_token_rows(0)}
         weight_rows = [load_weight_rows(side) for side in range(SIDES)]
+        nc.sync.dma_start(out=gains[:, 0, :], in_=w_q_norm.partition_broadcast(P))
+        nc.sync.dma_start(out=gains[:, 1, :], in_=w_k_norm.partition_broadcast(P))
         token_rows[1] = load_token_rows(1)
 
         token_codes = {0: new_token_codes(0)}
-        quantise_rows(gather_words(transpose_rows(token_rows[0]), 0), token_codes[0][0][:], token_codes[0][1][:])
+        grouped_rows = gather_words(transpose_rows(token_rows[0]), 0, nc.vector.tensor_copy)
+        quantise_rows(grouped_rows, token_codes[0][0][:], token_codes[0][1][:])
         for side in range(SIDES):
             side_cols = slice(side * SIDE_COLS, (side + 1) * SIDE_COLS)
-            grouped_rows = gather_words(transpose_rows(weight_rows[side]), 1 + side)
+            grouped_rows = gather_words(transpose_rows(weight_rows[side]), 1 + side, nc.vector.tensor_copy)
             quantise_rows(grouped_rows, w_codes[:, side_cols], w_scales[:, side_cols])
 
         pairs = BATCH * GROUPS // 2
+        batch_pairs = GROUPS // 2
         sums, sumsq, inv_rms, rows, grouped_qk = {}, {}, {}, {}, {}
-        for s in range(pairs + 3):
-            b, step = divmod(s, GROUPS // 2)
+        for s in range(pairs + 1):
+            b, step = divmod(s, batch_pairs)
             if s < pairs:
                 sumsq[s] = sbuf_ring("sumsq", s, 4, [P, 2, TOKEN_TILES], F32)
             for i in range(2):
@@ -227,33 +239,35 @@ def tile_transposedattentiontransformer_pa_t_kernel(tc, h, w_qk, w_q_norm, w_k_n
                     unit = 2 * s + i
                     sums[unit] = project(token_codes[b][0], token_codes[b][1], unit % GROUPS, unit)
                     sum_squares(sums[unit], unit, sumsq[s])
-                if i == 0 and 1 <= s <= pairs:
+                if i == 0 and s >= 1:
                     inv_rms[s - 1] = inverse_rms(sumsq[s - 1], s - 1)
-            if s < pairs and b + 1 < BATCH:
+            if b + 1 < BATCH:
                 if step == 0:
                     banks = transpose_rows(token_rows[b + 1])
                     if b + 2 < BATCH:
                         token_rows[b + 2] = load_token_rows(b + 2)
                 if step == 1:
-                    grouped_rows = gather_words(banks, b + 1)
-                if step == 2:
-                    token_codes[b + 1] = new_token_codes(b + 1)
-                    quantise_rows(grouped_rows, token_codes[b + 1][0][:], token_codes[b + 1][1][:])
-            if 1 <= s <= pairs:
-                index, half = divmod(s - 1, 2)
-                if half == 0:
-                    rows[index] = sbuf_ring("rows_qk", index, 3, [P, TOKEN_TILES, SIDE_COLS], BF16)
-                    grouped_qk[index] = sbuf_ring("grouped_qk", index, 3, [P, SIDE_COLS, PACK], BF16)
+                    grouped_rows = gather_words(banks, b + 1, nc.scalar.copy)
+            if s >= 1:
+                done_b, done_step = divmod(s - 1, batch_pairs)
+                if done_step == 0:
+                    rows[done_b] = sbuf_ring("rows_qk", done_b, 2, [P, TOKEN_TILES, QK_COLS], BF16)
+                    grouped_qk[done_b] = sbuf_ring("grouped_qk", done_b, 2, [P, QK_COLS, PACK], BF16)
                 for unit in (2 * s - 2, 2 * s - 1):
-                    normalise(sums[unit], inv_rms[s - 1], unit, rows[index])
-                    interleave(rows[index], grouped_qk[index], unit)
-            if s >= 4 and s % 2 == 0:
-                quantise_qk(grouped_qk[s // 2 - 2], s // 2 - 2)
+                    normalise(sums[unit], inv_rms[s - 1], unit, rows[done_b])
+                    interleave(rows[done_b], grouped_qk[done_b], unit)
+            if step == 2 and b + 1 < BATCH:
+                token_codes[b + 1] = new_token_codes(b + 1)
+                quantise_rows(grouped_rows, token_codes[b + 1][0][:], token_codes[b + 1][1][:])
+            if step == 2 and b >= 1:
+                quantise_qk(grouped_qk[b - 1], b - 1)
 
-        waiting = {0: scores(0)}
+        waiting = {b: scores(b) for b in range(2)}
         for b in range(BATCH):
-            if b + 1 < BATCH:
-                waiting[b + 1] = scores(b + 1)
+            if b + 2 < BATCH:
+                waiting[b + 2] = scores(b + 2)
             att, shift = waiting[b]
             weights, total = exponentials(att, shift, b)
             divide_and_store(weights, total, b)
+            if b == 0:
+                quantise_qk(grouped_qk[BATCH - 1], BATCH - 1)

@@ -27,7 +27,7 @@ TOKEN_TILES = TOKENS // P
 SIDE_COLS = HEADS * HEAD_DIM
 QK_COLS = SIDES * SIDE_COLS
 GROUPS = SIDES * HEADS
-SUM_BANKS = 6
+PSUM_BANKS = 8
 
 FLOPS = 2 * BATCH * TOKENS * CHANNELS * QK_COLS + 2 * BATCH * HEADS * HEAD_DIM * HEAD_DIM * TOKENS
 
@@ -43,8 +43,12 @@ def tile_transposedattentiontransformer_pa_t_kernel(tc, h, w_qk, w_q_norm, w_k_n
         def sbuf_ring(label, index, depth, shape, dtype):
             return sbuf.tile(shape, dtype, name=label, tag="%s_%d" % (label, index % depth), align_bytes=64)
 
-        def psum_ring(label, index, depth, shape):
-            return psum.tile(shape, F32, name=label, tag="%s_%d" % (label, index % depth))
+        banks_taken = []
+
+        def next_bank(shape):
+            bank = psum.tile(shape, F32, name="bank", tag="bank_%d" % (len(banks_taken) % PSUM_BANKS))
+            banks_taken.append(bank)
+            return bank
 
         ident = const.tile([P, P], F32)
         make_identity(nc, ident[:])
@@ -76,7 +80,7 @@ def tile_transposedattentiontransformer_pa_t_kernel(tc, h, w_qk, w_q_norm, w_k_n
             words = rows_sb[:].bitcast(F32)
             banks = []
             for n in range(2):
-                turned = psum_ring("turned", n, 2, [P, 4, P])
+                turned = next_bank([P, 4, P])
                 for i in range(4):
                     block = 4 * n + i
                     nc.tensor.transpose(turned[:, i, :], words[:, block * P : (block + 1) * P], ident[:])
@@ -98,9 +102,9 @@ def tile_transposedattentiontransformer_pa_t_kernel(tc, h, w_qk, w_q_norm, w_k_n
             h_scales = sbuf_ring("h_scales", b, 2, [P, TOKENS], U8)
             return h_codes, h_scales
 
-        def project(h_codes, h_scales, group, unit):
+        def project(h_codes, h_scales, group):
             group_cols = slice(group * HEAD_DIM, (group + 1) * HEAD_DIM)
-            sums = psum_ring("sums", unit, SUM_BANKS, [P, TOKEN_TILES, HEAD_DIM])
+            sums = next_bank([P, TOKEN_TILES, HEAD_DIM])
             for t in range(TOKEN_TILES):
                 token_cols = slice(t * P, (t + 1) * P)
                 nc.tensor.matmul_mx(
@@ -144,26 +148,28 @@ def tile_transposedattentiontransformer_pa_t_kernel(tc, h, w_qk, w_q_norm, w_k_n
                     op1=ALU.mult,
                 )
 
-        def interleave(rows, grouped, unit):
-            head_cols = slice((unit % GROUPS) * HEAD_DIM, (unit % GROUPS + 1) * HEAD_DIM)
+        def interleave(rows, grouped, pair):
+            step = pair % (GROUPS // 2)
+            pair_cols = slice(2 * step * HEAD_DIM, 2 * (step + 1) * HEAD_DIM)
             nc.gpsimd.tensor_scalar(
-                out=grouped[:, head_cols, :],
-                in0=rows[:, :, head_cols].rearrange("p t c -> p c t"),
+                out=grouped[:, pair_cols, :],
+                in0=rows[:, :, pair_cols].rearrange("p t c -> p c t"),
                 scalar1=1.0,
                 scalar2=0.0,
                 op0=ALU.mult,
                 op1=ALU.add,
             )
 
-        def quantise_qk(grouped, b):
+        def quantise_qk(grouped, b, side):
+            cols = slice(side * SIDE_COLS, (side + 1) * SIDE_COLS)
             nc.vector.quantize_mx(
-                out=qk_codes[:, b, :].bitcast(FP8X4),
-                scales=qk_scales[:, b, :],
-                in_=grouped[:].rearrange("p c t -> p (c t)"),
+                out=qk_codes[:, b, cols].bitcast(FP8X4),
+                scales=qk_scales[:, b, cols],
+                in_=grouped[:, cols, :].rearrange("p c t -> p (c t)"),
             )
 
         def scores(b):
-            att = psum_ring("sums", GROUPS * BATCH + b, SUM_BANKS, [P, HEADS, HEAD_DIM])
+            att = next_bank([P, HEADS, HEAD_DIM])
             for g in range(HEADS):
                 q_cols = slice(g * HEAD_DIM, (g + 1) * HEAD_DIM)
                 k_cols = slice(SIDE_COLS + g * HEAD_DIM, SIDE_COLS + (g + 1) * HEAD_DIM)
@@ -178,11 +184,12 @@ def tile_transposedattentiontransformer_pa_t_kernel(tc, h, w_qk, w_q_norm, w_k_n
                 )
             top = sbuf_ring("top", b, 4, [P, HEADS], F32)
             nc.vector.tensor_reduce(out=top[:], in_=att[:], axis=mybir.AxisListType.X, op=ALU.max)
+            return att, top
+
+        def exponent_shift(top, b):
             shift = sbuf_ring("shift", b, 4, [P, HEADS], F32)
-            nc.gpsimd.tensor_scalar(
-                out=shift[:], in0=top[:], scalar1=-SOFTMAX_SCALE, scalar2=0.0, op0=ALU.mult, op1=ALU.add
-            )
-            return att, shift
+            nc.vector.tensor_scalar_mul(out=shift[:], in0=top[:], scalar1=-SOFTMAX_SCALE)
+            return shift
 
         def exponentials(att, shift, b):
             weights = sbuf_ring("weights", b, 4, [P, HEADS, HEAD_DIM], F32)
@@ -198,9 +205,12 @@ def tile_transposedattentiontransformer_pa_t_kernel(tc, h, w_qk, w_q_norm, w_k_n
                 )
             return weights, total
 
-        def divide_and_store(weights, total, b):
+        def invert_total(total, b):
             inv_total = sbuf_ring("inv_total", b, 4, [P, HEADS], F32)
             nc.vector.reciprocal(out=inv_total[:], in_=total[:])
+            return inv_total
+
+        def divide_and_store(weights, inv_total, b):
             for g in range(HEADS):
                 engine = nc.vector if g < HEADS // 2 else nc.gpsimd
                 engine.tensor_scalar(
@@ -217,7 +227,8 @@ def tile_transposedattentiontransformer_pa_t_kernel(tc, h, w_qk, w_q_norm, w_k_n
         weight_rows = [load_weight_rows(side) for side in range(SIDES)]
         nc.sync.dma_start(out=gains[:, 0, :], in_=w_q_norm.partition_broadcast(P))
         nc.sync.dma_start(out=gains[:, 1, :], in_=w_k_norm.partition_broadcast(P))
-        token_rows[1] = load_token_rows(1)
+        for b in (1, 2):
+            token_rows[b] = load_token_rows(b)
 
         token_codes = {0: new_token_codes(0)}
         grouped_rows = gather_words(transpose_rows(token_rows[0]), 0, nc.vector.tensor_copy)
@@ -226,28 +237,35 @@ def tile_transposedattentiontransformer_pa_t_kernel(tc, h, w_qk, w_q_norm, w_k_n
             side_cols = slice(side * SIDE_COLS, (side + 1) * SIDE_COLS)
             grouped_rows = gather_words(transpose_rows(weight_rows[side]), 1 + side, nc.vector.tensor_copy)
             quantise_rows(grouped_rows, w_codes[:, side_cols], w_scales[:, side_cols])
+        turned = transpose_rows(token_rows[1])
 
         pairs = BATCH * GROUPS // 2
         batch_pairs = GROUPS // 2
         sums, sumsq, inv_rms, rows, grouped_qk = {}, {}, {}, {}, {}
         for s in range(pairs + 1):
             b, step = divmod(s, batch_pairs)
+            if step == 0 and b + 1 < BATCH:
+                grouped_rows = gather_words(turned, b + 1, nc.scalar.copy)
             if s < pairs:
                 sumsq[s] = sbuf_ring("sumsq", s, 4, [P, 2, TOKEN_TILES], F32)
             for i in range(2):
                 if s < pairs:
                     unit = 2 * s + i
-                    sums[unit] = project(token_codes[b][0], token_codes[b][1], unit % GROUPS, unit)
+                    sums[unit] = project(token_codes[b][0], token_codes[b][1], unit % GROUPS)
                     sum_squares(sums[unit], unit, sumsq[s])
                 if i == 0 and s >= 1:
                     inv_rms[s - 1] = inverse_rms(sumsq[s - 1], s - 1)
-            if b + 1 < BATCH:
-                if step == 0:
-                    banks = transpose_rows(token_rows[b + 1])
-                    if b + 2 < BATCH:
-                        token_rows[b + 2] = load_token_rows(b + 2)
-                if step == 1:
-                    grouped_rows = gather_words(banks, b + 1, nc.scalar.copy)
+            if step == batch_pairs - 1 and b + 2 < BATCH:
+                turned = transpose_rows(token_rows[b + 2])
+                if b + 3 < BATCH:
+                    token_rows[b + 3] = load_token_rows(b + 3)
+            if step == 0 and b >= 1:
+                quantise_qk(grouped_qk[b - 1], b - 1, 0)
+            if step == 1 and b + 1 < BATCH:
+                token_codes[b + 1] = new_token_codes(b + 1)
+                quantise_rows(grouped_rows, token_codes[b + 1][0][:], token_codes[b + 1][1][:])
+            if step == 2 and b >= 1:
+                quantise_qk(grouped_qk[b - 1], b - 1, 1)
             if s >= 1:
                 done_b, done_step = divmod(s - 1, batch_pairs)
                 if done_step == 0:
@@ -255,19 +273,20 @@ def tile_transposedattentiontransformer_pa_t_kernel(tc, h, w_qk, w_q_norm, w_k_n
                     grouped_qk[done_b] = sbuf_ring("grouped_qk", done_b, 2, [P, QK_COLS, PACK], BF16)
                 for unit in (2 * s - 2, 2 * s - 1):
                     normalise(sums[unit], inv_rms[s - 1], unit, rows[done_b])
-                    interleave(rows[done_b], grouped_qk[done_b], unit)
-            if step == 2 and b + 1 < BATCH:
-                token_codes[b + 1] = new_token_codes(b + 1)
-                quantise_rows(grouped_rows, token_codes[b + 1][0][:], token_codes[b + 1][1][:])
-            if step == 2 and b >= 1:
-                quantise_qk(grouped_qk[b - 1], b - 1)
+                interleave(rows[done_b], grouped_qk[done_b], s - 1)
 
-        waiting = {b: scores(b) for b in range(2)}
+        att, top, shift = {}, {}, {}
+        for b in range(2):
+            att[b], top[b] = scores(b)
+        for b in range(2):
+            shift[b] = exponent_shift(top[b], b)
         for b in range(BATCH):
             if b + 2 < BATCH:
-                waiting[b + 2] = scores(b + 2)
-            att, shift = waiting[b]
-            weights, total = exponentials(att, shift, b)
-            divide_and_store(weights, total, b)
+                att[b + 2], top[b + 2] = scores(b + 2)
+            weights, total = exponentials(att[b], shift[b], b)
+            inv_total = invert_total(total, b)
+            if b + 2 < BATCH:
+                shift[b + 2] = exponent_shift(top[b + 2], b + 2)
+            divide_and_store(weights, inv_total, b)
             if b == 0:
-                quantise_qk(grouped_qk[BATCH - 1], BATCH - 1)
+                quantise_qk(grouped_qk[BATCH - 1], BATCH - 1, 1)

@@ -135,10 +135,10 @@ def tile_transposedattentiontransformer_pa_t_kernel(tc, h, w_qk, w_q_norm, w_k_n
             )
             return inv_rms
 
-        def normalise(sums, inv_rms, unit, rows):
+        def normalise(sums, inv_rms, unit, rows, tokens):
             side = (unit % GROUPS) // HEADS
             head_cols = slice((unit % GROUPS) * HEAD_DIM, (unit % GROUPS + 1) * HEAD_DIM)
-            for t in range(TOKEN_TILES):
+            for t in tokens:
                 nc.vector.scalar_tensor_tensor(
                     out=rows[:, t, head_cols],
                     in0=sums[:, t, :],
@@ -259,6 +259,13 @@ def tile_transposedattentiontransformer_pa_t_kernel(tc, h, w_qk, w_q_norm, w_k_n
                 turned = transpose_rows(token_rows[b + 2])
                 if b + 3 < BATCH:
                     token_rows[b + 3] = load_token_rows(b + 3)
+            if s >= 1:
+                done_b, done_step = divmod(s - 1, batch_pairs)
+                if done_step == 0:
+                    rows[done_b] = sbuf_ring("rows_qk", done_b, 2, [P, TOKEN_TILES, QK_COLS], BF16)
+                    grouped_qk[done_b] = sbuf_ring("grouped_qk", done_b, 2, [P, QK_COLS, PACK], BF16)
+                normalise(sums[2 * s - 2], inv_rms[s - 1], 2 * s - 2, rows[done_b], range(TOKEN_TILES))
+                normalise(sums[2 * s - 1], inv_rms[s - 1], 2 * s - 1, rows[done_b], range(TOKEN_TILES - 1))
             if step == 0 and b >= 1:
                 quantise_qk(grouped_qk[b - 1], b - 1, 0)
             if step == 1 and b + 1 < BATCH:
@@ -267,12 +274,7 @@ def tile_transposedattentiontransformer_pa_t_kernel(tc, h, w_qk, w_q_norm, w_k_n
             if step == 2 and b >= 1:
                 quantise_qk(grouped_qk[b - 1], b - 1, 1)
             if s >= 1:
-                done_b, done_step = divmod(s - 1, batch_pairs)
-                if done_step == 0:
-                    rows[done_b] = sbuf_ring("rows_qk", done_b, 2, [P, TOKEN_TILES, QK_COLS], BF16)
-                    grouped_qk[done_b] = sbuf_ring("grouped_qk", done_b, 2, [P, QK_COLS, PACK], BF16)
-                for unit in (2 * s - 2, 2 * s - 1):
-                    normalise(sums[unit], inv_rms[s - 1], unit, rows[done_b])
+                normalise(sums[2 * s - 1], inv_rms[s - 1], 2 * s - 1, rows[done_b], range(TOKEN_TILES - 1, TOKEN_TILES))
                 interleave(rows[done_b], grouped_qk[done_b], s - 1)
 
         att, top, shift = {}, {}, {}

@@ -63,9 +63,12 @@ def tile_transposedattentiontransformer_pa_t_kernel(tc, h, w_qk, w_q_norm, w_k_n
         qk_codes = const.tile([P, BATCH, QK_COLS], U32, align_bytes=64)
         qk_scales = const.tile([P, BATCH, QK_COLS], U8, align_bytes=64)
 
-        def load_token_rows(b):
+        def load_token_rows(b, pieces):
             rows_sb = sbuf_ring("token_rows", b, 3, [P, ROW_TILES * CHANNELS], BF16)
-            nc.sync.dma_start(out=rows_sb[:], in_=h[b].rearrange("(p t) c -> p (t c)", t=ROW_TILES))
+            run = ROW_TILES * CHANNELS // pieces
+            for i in range(pieces):
+                piece = slice(i * run, (i + 1) * run)
+                nc.sync.dma_start(out=rows_sb[:, piece], in_=h[b].rearrange("(p t) c -> p (t c)", t=ROW_TILES)[:, piece])
             return rows_sb
 
         def load_weight_rows(side):
@@ -87,10 +90,10 @@ def tile_transposedattentiontransformer_pa_t_kernel(tc, h, w_qk, w_q_norm, w_k_n
                 banks.append(turned)
             return banks
 
-        def gather_words(banks, call, second_copy):
+        def gather_words(banks, call, copies):
             grouped = sbuf_ring("grouped_rows", call, 2, [P, ROW_TILES * P * PACK], BF16)
             pairs = grouped[:].bitcast(F32).rearrange("p (n r k u) -> p n r k u", n=2, r=2, u=2)
-            for n, copy in enumerate((nc.scalar.copy, second_copy)):
+            for n, copy in enumerate(copies):
                 copy(out=pairs[:, n], in_=banks[n][:].rearrange("p (r u) k -> p r k u", u=2))
             return grouped
 
@@ -160,12 +163,11 @@ def tile_transposedattentiontransformer_pa_t_kernel(tc, h, w_qk, w_q_norm, w_k_n
                 op1=ALU.add,
             )
 
-        def quantise_qk(grouped, b, side):
-            cols = slice(side * SIDE_COLS, (side + 1) * SIDE_COLS)
+        def quantise_qk(grouped, b):
             nc.vector.quantize_mx(
-                out=qk_codes[:, b, cols].bitcast(FP8X4),
-                scales=qk_scales[:, b, cols],
-                in_=grouped[:, cols, :].rearrange("p c t -> p (c t)"),
+                out=qk_codes[:, b, :].bitcast(FP8X4),
+                scales=qk_scales[:, b, :],
+                in_=grouped[:].rearrange("p c t -> p (c t)"),
             )
 
         def scores(b):
@@ -223,19 +225,22 @@ def tile_transposedattentiontransformer_pa_t_kernel(tc, h, w_qk, w_q_norm, w_k_n
                 )
             nc.sync.dma_start(out=out[b].rearrange("g d e -> d g e"), in_=weights[:])
 
-        token_rows = {0: load_token_rows(0)}
+        token_rows = {0: load_token_rows(0, 2)}
         weight_rows = [load_weight_rows(side) for side in range(SIDES)]
         nc.sync.dma_start(out=gains[:, 0, :], in_=w_q_norm.partition_broadcast(P))
         nc.sync.dma_start(out=gains[:, 1, :], in_=w_k_norm.partition_broadcast(P))
         for b in (1, 2):
-            token_rows[b] = load_token_rows(b)
+            token_rows[b] = load_token_rows(b, 1)
 
+        both_engines = (nc.scalar.copy, nc.vector.tensor_copy)
+        vector_alone = (nc.vector.tensor_copy, nc.vector.tensor_copy)
         token_codes = {0: new_token_codes(0)}
-        grouped_rows = gather_words(transpose_rows(token_rows[0]), 0, nc.vector.tensor_copy)
+        grouped_rows = gather_words(transpose_rows(token_rows[0]), 0, both_engines)
         quantise_rows(grouped_rows, token_codes[0][0][:], token_codes[0][1][:])
         for side in range(SIDES):
             side_cols = slice(side * SIDE_COLS, (side + 1) * SIDE_COLS)
-            grouped_rows = gather_words(transpose_rows(weight_rows[side]), 1 + side, nc.vector.tensor_copy)
+            copies = both_engines if side == 0 else vector_alone
+            grouped_rows = gather_words(transpose_rows(weight_rows[side]), 1 + side, copies)
             quantise_rows(grouped_rows, w_codes[:, side_cols], w_scales[:, side_cols])
         turned = transpose_rows(token_rows[1])
 
@@ -245,7 +250,7 @@ def tile_transposedattentiontransformer_pa_t_kernel(tc, h, w_qk, w_q_norm, w_k_n
         for s in range(pairs + 1):
             b, step = divmod(s, batch_pairs)
             if step == 0 and b + 1 < BATCH:
-                grouped_rows = gather_words(turned, b + 1, nc.scalar.copy)
+                grouped_rows = gather_words(turned, b + 1, (nc.scalar.copy, nc.scalar.copy))
             if s < pairs:
                 sumsq[s] = sbuf_ring("sumsq", s, 4, [P, 2, TOKEN_TILES], F32)
             for i in range(2):
@@ -258,7 +263,7 @@ def tile_transposedattentiontransformer_pa_t_kernel(tc, h, w_qk, w_q_norm, w_k_n
             if step == batch_pairs - 1 and b + 2 < BATCH:
                 turned = transpose_rows(token_rows[b + 2])
                 if b + 3 < BATCH:
-                    token_rows[b + 3] = load_token_rows(b + 3)
+                    token_rows[b + 3] = load_token_rows(b + 3, 1)
             if s >= 1:
                 done_b, done_step = divmod(s - 1, batch_pairs)
                 if done_step == 0:
@@ -266,13 +271,11 @@ def tile_transposedattentiontransformer_pa_t_kernel(tc, h, w_qk, w_q_norm, w_k_n
                     grouped_qk[done_b] = sbuf_ring("grouped_qk", done_b, 2, [P, QK_COLS, PACK], BF16)
                 normalise(sums[2 * s - 2], inv_rms[s - 1], 2 * s - 2, rows[done_b], range(TOKEN_TILES))
                 normalise(sums[2 * s - 1], inv_rms[s - 1], 2 * s - 1, rows[done_b], range(TOKEN_TILES - 1))
-            if step == 0 and b >= 1:
-                quantise_qk(grouped_qk[b - 1], b - 1, 0)
             if step == 1 and b + 1 < BATCH:
                 token_codes[b + 1] = new_token_codes(b + 1)
                 quantise_rows(grouped_rows, token_codes[b + 1][0][:], token_codes[b + 1][1][:])
-            if step == 2 and b >= 1:
-                quantise_qk(grouped_qk[b - 1], b - 1, 1)
+            if step == 1 and b >= 1:
+                quantise_qk(grouped_qk[b - 1], b - 1)
             if s >= 1:
                 normalise(sums[2 * s - 1], inv_rms[s - 1], 2 * s - 1, rows[done_b], range(TOKEN_TILES - 1, TOKEN_TILES))
                 interleave(rows[done_b], grouped_qk[done_b], s - 1)
@@ -291,4 +294,4 @@ def tile_transposedattentiontransformer_pa_t_kernel(tc, h, w_qk, w_q_norm, w_k_n
                 shift[b + 2] = exponent_shift(top[b + 2], b + 2)
             divide_and_store(weights, inv_total, b)
             if b == 0:
-                quantise_qk(grouped_qk[BATCH - 1], BATCH - 1, 1)
+                quantise_qk(grouped_qk[BATCH - 1], BATCH - 1)

@@ -151,12 +151,10 @@ def tile_transposedattentiontransformer_pa_t_kernel(tc, h, w_qk, w_q_norm, w_k_n
                     op1=ALU.mult,
                 )
 
-        def interleave(rows, grouped, pair):
-            step = pair % (GROUPS // 2)
-            pair_cols = slice(2 * step * HEAD_DIM, 2 * (step + 1) * HEAD_DIM)
+        def interleave(rows, grouped, cols):
             nc.gpsimd.tensor_scalar(
-                out=grouped[:, pair_cols, :],
-                in0=rows[:, :, pair_cols].rearrange("p t c -> p c t"),
+                out=grouped[:, cols, :],
+                in0=rows[:, :, cols].rearrange("p t c -> p c t"),
                 scalar1=1.0,
                 scalar2=0.0,
                 op0=ALU.mult,
@@ -186,15 +184,14 @@ def tile_transposedattentiontransformer_pa_t_kernel(tc, h, w_qk, w_q_norm, w_k_n
                 )
             top = sbuf_ring("top", b, 4, [P, HEADS], F32)
             nc.vector.tensor_reduce(out=top[:], in_=att[:], axis=mybir.AxisListType.X, op=ALU.max)
-            return att, top
-
-        def exponent_shift(top, b):
             shift = sbuf_ring("shift", b, 4, [P, HEADS], F32)
-            nc.vector.tensor_scalar_mul(out=shift[:], in0=top[:], scalar1=-SOFTMAX_SCALE)
-            return shift
+            nc.gpsimd.tensor_scalar(
+                out=shift[:], in0=top[:], scalar1=-SOFTMAX_SCALE, scalar2=0.0, op0=ALU.mult, op1=ALU.add
+            )
+            return att, shift
 
         def exponentials(att, shift, b):
-            weights = sbuf_ring("weights", b, 4, [P, HEADS, HEAD_DIM], F32)
+            weights = sbuf_ring("weights", b, 6, [P, HEADS, HEAD_DIM], F32)
             total = sbuf_ring("total", b, 4, [P, HEADS], F32)
             for g in range(HEADS):
                 nc.scalar.activation(
@@ -212,10 +209,9 @@ def tile_transposedattentiontransformer_pa_t_kernel(tc, h, w_qk, w_q_norm, w_k_n
             nc.vector.reciprocal(out=inv_total[:], in_=total[:])
             return inv_total
 
-        def divide_and_store(weights, inv_total, b):
-            for g in range(HEADS):
-                engine = nc.vector if g < HEADS // 2 else nc.gpsimd
-                engine.tensor_scalar(
+        def divide_on_gpsimd(weights, inv_total):
+            for g in range(HEADS // 2):
+                nc.gpsimd.tensor_scalar(
                     out=weights[:, g, :],
                     in0=weights[:, g, :],
                     scalar1=inv_total[:, g : g + 1],
@@ -223,6 +219,16 @@ def tile_transposedattentiontransformer_pa_t_kernel(tc, h, w_qk, w_q_norm, w_k_n
                     op0=ALU.mult,
                     op1=ALU.add,
                 )
+
+        def divide_on_vector_and_scalar(weights, inv_total):
+            g = HEADS - 2
+            nc.vector.tensor_scalar_mul(out=weights[:, g, :], in0=weights[:, g, :], scalar1=inv_total[:, g : g + 1])
+            g = HEADS - 1
+            nc.scalar.activation(
+                out=weights[:, g, :], in_=weights[:, g, :], func=ACT.Copy, scale=inv_total[:, g : g + 1]
+            )
+
+        def store(weights, b):
             nc.sync.dma_start(out=out[b].rearrange("g d e -> d g e"), in_=weights[:])
 
         token_rows = {0: load_token_rows(0, 2)}
@@ -264,6 +270,8 @@ def tile_transposedattentiontransformer_pa_t_kernel(tc, h, w_qk, w_q_norm, w_k_n
                 turned = transpose_rows(token_rows[b + 2])
                 if b + 3 < BATCH:
                     token_rows[b + 3] = load_token_rows(b + 3, 1)
+            if s == pairs - 1:
+                waiting = {0: scores(0)}
             if s >= 1:
                 done_b, done_step = divmod(s - 1, batch_pairs)
                 if done_step == 0:
@@ -271,27 +279,32 @@ def tile_transposedattentiontransformer_pa_t_kernel(tc, h, w_qk, w_q_norm, w_k_n
                     grouped_qk[done_b] = sbuf_ring("grouped_qk", done_b, 2, [P, QK_COLS, PACK], BF16)
                 normalise(sums[2 * s - 2], inv_rms[s - 1], 2 * s - 2, rows[done_b], range(TOKEN_TILES))
                 normalise(sums[2 * s - 1], inv_rms[s - 1], 2 * s - 1, rows[done_b], range(TOKEN_TILES - 1))
-            if step == 1 and b + 1 < BATCH:
-                token_codes[b + 1] = new_token_codes(b + 1)
-                quantise_rows(grouped_rows, token_codes[b + 1][0][:], token_codes[b + 1][1][:])
-            if step == 1 and b >= 1:
-                quantise_qk(grouped_qk[b - 1], b - 1)
-            if s >= 1:
+                if done_step == 1 and done_b + 1 < BATCH:
+                    token_codes[done_b + 1] = new_token_codes(done_b + 1)
+                    quantise_rows(grouped_rows, token_codes[done_b + 1][0][:], token_codes[done_b + 1][1][:])
+                if done_step == 1 and done_b >= 1:
+                    quantise_qk(grouped_qk[done_b - 1], done_b - 1)
                 normalise(sums[2 * s - 1], inv_rms[s - 1], 2 * s - 1, rows[done_b], range(TOKEN_TILES - 1, TOKEN_TILES))
-                interleave(rows[done_b], grouped_qk[done_b], s - 1)
+            if s == pairs:
+                waiting[1] = scores(1)
+            if s >= 1:
+                last_keys = done_b == BATCH - 1 and done_step >= 2
+                if last_keys or done_step % 2 == 1:
+                    pairs_at_once = 1 if last_keys else 2
+                    end = 2 * (done_step + 1) * HEAD_DIM
+                    interleave(rows[done_b], grouped_qk[done_b], slice(end - 2 * pairs_at_once * HEAD_DIM, end))
 
-        att, top, shift = {}, {}, {}
-        for b in range(2):
-            att[b], top[b] = scores(b)
-        for b in range(2):
-            shift[b] = exponent_shift(top[b], b)
         for b in range(BATCH):
             if b + 2 < BATCH:
-                att[b + 2], top[b + 2] = scores(b + 2)
-            weights, total = exponentials(att[b], shift[b], b)
+                waiting[b + 2] = scores(b + 2)
+            weights, total = exponentials(waiting[b][0], waiting[b][1], b)
             inv_total = invert_total(total, b)
-            if b + 2 < BATCH:
-                shift[b + 2] = exponent_shift(top[b + 2], b + 2)
-            divide_and_store(weights, inv_total, b)
+            divide_on_gpsimd(weights, inv_total)
+            if b > 0:
+                divide_on_vector_and_scalar(last_weights, last_inv_total)
+                store(last_weights, b - 1)
+            last_weights, last_inv_total = weights, inv_total
             if b == 0:
                 quantise_qk(grouped_qk[BATCH - 1], BATCH - 1)
+        divide_on_vector_and_scalar(last_weights, last_inv_total)
+        store(last_weights, BATCH - 1)

@@ -27,6 +27,7 @@ TOKEN_TILES = TOKENS // P
 SIDE_COLS = HEADS * HEAD_DIM
 QK_COLS = SIDES * SIDE_COLS
 GROUPS = SIDES * HEADS
+DEFERRED = 4
 PSUM_BANKS = 8
 
 FLOPS = 2 * BATCH * TOKENS * CHANNELS * QK_COLS + 2 * BATCH * HEADS * HEAD_DIM * HEAD_DIM * TOKENS
@@ -71,12 +72,14 @@ def tile_transposedattentiontransformer_pa_t_kernel(tc, h, w_qk, w_q_norm, w_k_n
                 nc.sync.dma_start(out=rows_sb[:, piece], in_=h[b].rearrange("(p t) c -> p (t c)", t=ROW_TILES)[:, piece])
             return rows_sb
 
-        def load_weight_rows(side):
+        def load_weight_rows(side, pieces):
             rows_sb = sbuf_ring("weight_rows", side, SIDES, [P, ROW_TILES * CHANNELS], BF16)
-            nc.sync.dma_start(
-                out=rows_sb[:].rearrange("p (r c) -> p r c", r=ROW_TILES),
-                in_=w_qk[side * SIDE_COLS : (side + 1) * SIDE_COLS, :].rearrange("(r p) c -> p r c", p=P),
-            )
+            rows_out = rows_sb[:].rearrange("p (r c) -> p r c", r=ROW_TILES)
+            rows_in = w_qk[side * SIDE_COLS : (side + 1) * SIDE_COLS, :].rearrange("(r p) c -> p r c", p=P)
+            run = ROW_TILES // pieces
+            for i in range(pieces):
+                piece = slice(i * run, (i + 1) * run)
+                nc.sync.dma_start(out=rows_out[:, piece, :], in_=rows_in[:, piece, :])
             return rows_sb
 
         def transpose_rows(rows_sb):
@@ -98,7 +101,7 @@ def tile_transposedattentiontransformer_pa_t_kernel(tc, h, w_qk, w_q_norm, w_k_n
             return grouped
 
         def quantise_rows(grouped, codes, scales):
-            nc.vector.quantize_mx(out=codes.bitcast(FP8X4), scales=scales, in_=grouped[:])
+            nc.vector.quantize_mx(out=codes.bitcast(FP8X4), scales=scales, in_=grouped)
 
         def new_token_codes(b):
             h_codes = sbuf_ring("h_codes", b, 2, [P, TOKENS], U32)
@@ -131,12 +134,10 @@ def tile_transposedattentiontransformer_pa_t_kernel(tc, h, w_qk, w_q_norm, w_k_n
                     accum_out=sumsq[:, unit % 2, t : t + 1],
                 )
 
-        def inverse_rms(sumsq, pair):
-            inv_rms = sbuf_ring("inv_rms", pair, 4, [P, 2, TOKEN_TILES], F32)
+        def inverse_rms(inv_rms, sumsq):
             nc.scalar.activation(
-                out=inv_rms[:], in_=sumsq[:], func=ACT.Abs_reciprocal_sqrt, scale=1.0 / HEAD_DIM, bias=eps[:]
+                out=inv_rms, in_=sumsq, func=ACT.Abs_reciprocal_sqrt, scale=1.0 / HEAD_DIM, bias=eps[:]
             )
-            return inv_rms
 
         def normalise(sums, inv_rms, unit, rows, tokens):
             side = (unit % GROUPS) // HEADS
@@ -182,9 +183,9 @@ def tile_transposedattentiontransformer_pa_t_kernel(tc, h, w_qk, w_q_norm, w_k_n
                     start=True,
                     stop=True,
                 )
-            top = sbuf_ring("top", b, 4, [P, HEADS], F32)
+            top = sbuf_ring("top", b, 5, [P, HEADS], F32)
             nc.vector.tensor_reduce(out=top[:], in_=att[:], axis=mybir.AxisListType.X, op=ALU.max)
-            shift = sbuf_ring("shift", b, 4, [P, HEADS], F32)
+            shift = sbuf_ring("shift", b, 5, [P, HEADS], F32)
             nc.gpsimd.tensor_scalar(
                 out=shift[:], in0=top[:], scalar1=-SOFTMAX_SCALE, scalar2=0.0, op0=ALU.mult, op1=ALU.add
             )
@@ -220,52 +221,58 @@ def tile_transposedattentiontransformer_pa_t_kernel(tc, h, w_qk, w_q_norm, w_k_n
                     op1=ALU.add,
                 )
 
-        def divide_on_vector_and_scalar(weights, inv_total):
-            g = HEADS - 2
-            nc.vector.tensor_scalar_mul(out=weights[:, g, :], in0=weights[:, g, :], scalar1=inv_total[:, g : g + 1])
-            g = HEADS - 1
-            nc.scalar.activation(
-                out=weights[:, g, :], in_=weights[:, g, :], func=ACT.Copy, scale=inv_total[:, g : g + 1]
-            )
+        def divide_on_scalar(weights, inv_total):
+            for g in range(HEADS // 2, HEADS):
+                nc.scalar.activation(
+                    out=weights[:, g, :], in_=weights[:, g, :], func=ACT.Copy, scale=inv_total[:, g : g + 1]
+                )
 
         def store(weights, b):
             nc.sync.dma_start(out=out[b].rearrange("g d e -> d g e"), in_=weights[:])
 
         token_rows = {0: load_token_rows(0, 2)}
-        weight_rows = [load_weight_rows(side) for side in range(SIDES)]
+        weight_rows = [load_weight_rows(0, 2), load_weight_rows(1, 1)]
         nc.sync.dma_start(out=gains[:, 0, :], in_=w_q_norm.partition_broadcast(P))
         nc.sync.dma_start(out=gains[:, 1, :], in_=w_k_norm.partition_broadcast(P))
         for b in (1, 2):
             token_rows[b] = load_token_rows(b, 1)
 
         both_engines = (nc.scalar.copy, nc.vector.tensor_copy)
+        scalar_alone = (nc.scalar.copy, nc.scalar.copy)
         vector_alone = (nc.vector.tensor_copy, nc.vector.tensor_copy)
         token_codes = {0: new_token_codes(0)}
         grouped_rows = gather_words(transpose_rows(token_rows[0]), 0, both_engines)
-        quantise_rows(grouped_rows, token_codes[0][0][:], token_codes[0][1][:])
-        for side in range(SIDES):
-            side_cols = slice(side * SIDE_COLS, (side + 1) * SIDE_COLS)
-            copies = both_engines if side == 0 else vector_alone
-            grouped_rows = gather_words(transpose_rows(weight_rows[side]), 1 + side, copies)
-            quantise_rows(grouped_rows, w_codes[:, side_cols], w_scales[:, side_cols])
-        turned = transpose_rows(token_rows[1])
+        quantise_rows(grouped_rows[:], token_codes[0][0][:], token_codes[0][1][:])
+        half = SIDE_COLS // 2
+        grouped_rows = gather_words(transpose_rows(weight_rows[0]), 1, scalar_alone)
+        for i in range(2):
+            cols = slice(i * half, (i + 1) * half)
+            quantise_rows(grouped_rows[:, i * half * PACK : (i + 1) * half * PACK], w_codes[:, cols], w_scales[:, cols])
+        side_cols = slice(SIDE_COLS, QK_COLS)
+        grouped_rows = gather_words(transpose_rows(weight_rows[1]), 2, vector_alone)
+        quantise_rows(grouped_rows[:], w_codes[:, side_cols], w_scales[:, side_cols])
 
         pairs = BATCH * GROUPS // 2
         batch_pairs = GROUPS // 2
         sums, sumsq, inv_rms, rows, grouped_qk = {}, {}, {}, {}, {}
         for s in range(pairs + 1):
             b, step = divmod(s, batch_pairs)
-            if step == 0 and b + 1 < BATCH:
-                grouped_rows = gather_words(turned, b + 1, (nc.scalar.copy, nc.scalar.copy))
+            if s == 1:
+                turned = transpose_rows(token_rows[1])
+            if s == 2 or (step == 0 and 1 <= b < BATCH - 1):
+                grouped_rows = gather_words(turned, b + 1, scalar_alone)
             if s < pairs:
                 sumsq[s] = sbuf_ring("sumsq", s, 4, [P, 2, TOKEN_TILES], F32)
+                inv_rms[s] = sbuf_ring("inv_rms", s, 4, [P, 2, TOKEN_TILES], F32)
             for i in range(2):
                 if s < pairs:
                     unit = 2 * s + i
                     sums[unit] = project(token_codes[b][0], token_codes[b][1], unit % GROUPS)
                     sum_squares(sums[unit], unit, sumsq[s])
-                if i == 0 and s >= 1:
-                    inv_rms[s - 1] = inverse_rms(sumsq[s - 1], s - 1)
+                if s == 0:
+                    inverse_rms(inv_rms[0][:, i, :], sumsq[0][:, i, :])
+                elif i == 0 and s >= 2:
+                    inverse_rms(inv_rms[s - 1][:], sumsq[s - 1][:])
             if step == batch_pairs - 1 and b + 2 < BATCH:
                 turned = transpose_rows(token_rows[b + 2])
                 if b + 3 < BATCH:
@@ -276,13 +283,13 @@ def tile_transposedattentiontransformer_pa_t_kernel(tc, h, w_qk, w_q_norm, w_k_n
                 done_b, done_step = divmod(s - 1, batch_pairs)
                 if done_step == 0:
                     rows[done_b] = sbuf_ring("rows_qk", done_b, 2, [P, TOKEN_TILES, QK_COLS], BF16)
-                    grouped_qk[done_b] = sbuf_ring("grouped_qk", done_b, 2, [P, QK_COLS, PACK], BF16)
+                    grouped_qk[done_b] = sbuf_ring("grouped_qk", done_b, DEFERRED, [P, QK_COLS, PACK], BF16)
                 normalise(sums[2 * s - 2], inv_rms[s - 1], 2 * s - 2, rows[done_b], range(TOKEN_TILES))
                 normalise(sums[2 * s - 1], inv_rms[s - 1], 2 * s - 1, rows[done_b], range(TOKEN_TILES - 1))
                 if done_step == 1 and done_b + 1 < BATCH:
                     token_codes[done_b + 1] = new_token_codes(done_b + 1)
-                    quantise_rows(grouped_rows, token_codes[done_b + 1][0][:], token_codes[done_b + 1][1][:])
-                if done_step == 1 and done_b >= 1:
+                    quantise_rows(grouped_rows[:], token_codes[done_b + 1][0][:], token_codes[done_b + 1][1][:])
+                if done_step == 1 and 1 <= done_b <= BATCH - DEFERRED:
                     quantise_qk(grouped_qk[done_b - 1], done_b - 1)
                 normalise(sums[2 * s - 1], inv_rms[s - 1], 2 * s - 1, rows[done_b], range(TOKEN_TILES - 1, TOKEN_TILES))
             if s == pairs:
@@ -294,17 +301,19 @@ def tile_transposedattentiontransformer_pa_t_kernel(tc, h, w_qk, w_q_norm, w_k_n
                     end = 2 * (done_step + 1) * HEAD_DIM
                     interleave(rows[done_b], grouped_qk[done_b], slice(end - 2 * pairs_at_once * HEAD_DIM, end))
 
+        waiting[2] = scores(2)
         for b in range(BATCH):
-            if b + 2 < BATCH:
-                waiting[b + 2] = scores(b + 2)
+            if b + 3 < BATCH:
+                waiting[b + 3] = scores(b + 3)
             weights, total = exponentials(waiting[b][0], waiting[b][1], b)
             inv_total = invert_total(total, b)
             divide_on_gpsimd(weights, inv_total)
             if b > 0:
-                divide_on_vector_and_scalar(last_weights, last_inv_total)
+                divide_on_scalar(last_weights, last_inv_total)
                 store(last_weights, b - 1)
             last_weights, last_inv_total = weights, inv_total
-            if b == 0:
-                quantise_qk(grouped_qk[BATCH - 1], BATCH - 1)
-        divide_on_vector_and_scalar(last_weights, last_inv_total)
+            if b % 3 == 1 and b < 3 * DEFERRED:
+                deferred_b = BATCH - DEFERRED + b // 3
+                quantise_qk(grouped_qk[deferred_b], deferred_b)
+        divide_on_scalar(last_weights, last_inv_total)
         store(last_weights, BATCH - 1)

from contextlib import ExitStack

import concourse.mybir as mybir
from concourse.masks import make_identity

F32 = mybir.dt.float32
BF16 = mybir.dt.bfloat16
U32 = mybir.dt.uint32
U8 = mybir.dt.uint8
FP8X4 = mybir.dt.float8_e4m3fn_x4
ACT = mybir.ActivationFunctionType
ALU = mybir.AluOpType

P = 128
PACK = 4
BATCH = 16
TOKENS = 512
CHANNELS = 512
HEADS = 4
HEAD_DIM = 128
SIDES = 2
EPS = 1e-5
SOFTMAX_SCALE = HEAD_DIM**-0.5

ROW_TILES = 4
TOKEN_TILES = TOKENS // P
SIDE_COLS = HEADS * HEAD_DIM
QK_COLS = SIDES * SIDE_COLS
GROUPS = SIDES * HEADS
DEFERRED = 4
PSUM_BANKS = 8

FLOPS = 2 * BATCH * TOKENS * CHANNELS * QK_COLS + 2 * BATCH * HEADS * HEAD_DIM * HEAD_DIM * TOKENS


def tile_transposedattentiontransformer_pa_t_kernel(tc, h, w_qk, w_q_norm, w_k_norm, out):
    nc = tc.nc
    with ExitStack() as ctx:
        const = ctx.enter_context(tc.tile_pool(name="const", bufs=1))
        sbuf = ctx.enter_context(tc.tile_pool(name="sbuf", bufs=1))
        psum = ctx.enter_context(tc.psum_pool(name="psum", bufs=1))
        ctx.enter_context(tc.manual_schedule())

        def sbuf_ring(label, index, depth, shape, dtype):
            return sbuf.tile(shape, dtype, name=label, tag="%s_%d" % (label, index % depth), align_bytes=64)

        banks_taken = []

        def next_bank(shape):
            bank = psum.tile(shape, F32, name="bank", tag="bank_%d" % (len(banks_taken) % PSUM_BANKS))
            banks_taken.append(bank)
            return bank

        ident = const.tile([P, P], F32)
        make_identity(nc, ident[:])
        eps = const.tile([P, 1], F32)
        nc.vector.memset(eps[:], EPS)
        gains = const.tile([P, SIDES, HEAD_DIM], BF16)
        first_root = const.tile([P, 1], F32)
        nc.scalar.activation(out=first_root[:], in_=eps[:], func=ACT.Abs_reciprocal_sqrt)

        w_codes = const.tile([P, QK_COLS], U32, align_bytes=64)
        w_scales = const.tile([P, QK_COLS], U8, align_bytes=64)
        qk_codes = const.tile([P, BATCH, QK_COLS], U32, align_bytes=64)
        qk_scales = const.tile([P, BATCH, QK_COLS], U8, align_bytes=64)

        def load_token_rows(b, pieces):
            rows_sb = sbuf_ring("token_rows", b, 3, [P, ROW_TILES * CHANNELS], BF16)
            run = ROW_TILES * CHANNELS // pieces
            for i in range(pieces):
                piece = slice(i * run, (i + 1) * run)
                nc.sync.dma_start(out=rows_sb[:, piece], in_=h[b].rearrange("(p t) c -> p (t c)", t=ROW_TILES)[:, piece])
            return rows_sb

        def load_weight_rows(side, pieces):
            rows_sb = sbuf_ring("weight_rows", side, SIDES, [P, ROW_TILES * CHANNELS], BF16)
            rows_out = rows_sb[:].rearrange("p (r c) -> p r c", r=ROW_TILES)
            rows_in = w_qk[side * SIDE_COLS : (side + 1) * SIDE_COLS, :].rearrange("(r p) c -> p r c", p=P)
            run = ROW_TILES // pieces
            for i in range(pieces):
                piece = slice(i * run, (i + 1) * run)
                nc.sync.dma_start(out=rows_out[:, piece, :], in_=rows_in[:, piece, :])
            return rows_sb

        def transpose_rows(rows_sb):
            words = rows_sb[:].bitcast(F32)
            banks = []
            for n in range(2):
                turned = next_bank([P, 4, P])
                for i in range(4):
                    block = 4 * n + i
                    nc.tensor.transpose(turned[:, i, :], words[:, block * P : (block + 1) * P], ident[:])
                banks.append(turned)
            return banks

        def gather_words(banks, call, copies):
            grouped = sbuf_ring("grouped_rows", call, 2, [P, ROW_TILES * P * PACK], BF16)
            pairs = grouped[:].bitcast(F32).rearrange("p (n r k u) -> p n r k u", n=2, r=2, u=2)
            for n, copy in enumerate(copies):
                copy(out=pairs[:, n], in_=banks[n][:].rearrange("p (r u) k -> p r k u", u=2))
            return grouped

        def quantise_rows(grouped, codes, scales):
            nc.vector.quantize_mx(out=codes.bitcast(FP8X4), scales=scales, in_=grouped)

        def new_token_codes(b):
            h_codes = sbuf_ring("h_codes", b, 2, [P, TOKENS], U32)
            h_scales = sbuf_ring("h_scales", b, 2, [P, TOKENS], U8)
            return h_codes, h_scales

        def project(h_codes, h_scales, group):
            group_cols = slice(group * HEAD_DIM, (group + 1) * HEAD_DIM)
            sums = next_bank([P, TOKEN_TILES, HEAD_DIM])
            for t in range(TOKEN_TILES):
                token_cols = slice(t * P, (t + 1) * P)
                nc.tensor.matmul_mx(
                    out=sums[:, t, :],
                    lhsT=h_codes[:, token_cols].bitcast(FP8X4),
                    lhsT_scale=h_scales[:, token_cols],
                    rhs=w_codes[:, group_cols].bitcast(FP8X4),
                    rhs_scale=w_scales[:, group_cols],
                    start=True,
                    stop=True,
                )
            return sums

        def sum_squares(sums, unit, sumsq):
            squares = sbuf_ring("squares", unit, 4, [P, TOKEN_TILES, HEAD_DIM], F32)
            for t in range(TOKEN_TILES):
                nc.scalar.activation(
                    out=squares[:, t, :],
                    in_=sums[:, t, :],
                    func=ACT.Square,
                    accum_out=sumsq[:, unit % 2, t : t + 1],
                )

        def inverse_rms(inv_rms, sumsq):
            nc.scalar.activation(
                out=inv_rms, in_=sumsq, func=ACT.Abs_reciprocal_sqrt, scale=1.0 / HEAD_DIM, bias=eps[:]
            )

        def normalise(sums, inv_rms, unit, rows, tokens):
            side = (unit % GROUPS) // HEADS
            head_cols = slice((unit % GROUPS) * HEAD_DIM, (unit % GROUPS + 1) * HEAD_DIM)
            for t in tokens:
                nc.vector.scalar_tensor_tensor(
                    out=rows[:, t, head_cols],
                    in0=sums[:, t, :],
                    scalar=inv_rms[:, unit % 2, t : t + 1],
                    in1=gains[:, side, :],
                    op0=ALU.mult,
                    op1=ALU.mult,
                )

        def interleave(rows, grouped, cols):
            nc.gpsimd.tensor_scalar(
                out=grouped[:, cols, :],
                in0=rows[:, :, cols].rearrange("p t c -> p c t"),
                scalar1=1.0,
                scalar2=0.0,
                op0=ALU.mult,
                op1=ALU.add,
            )

        def quantise_qk(grouped, b):
            nc.vector.quantize_mx(
                out=qk_codes[:, b, :].bitcast(FP8X4),
                scales=qk_scales[:, b, :],
                in_=grouped[:].rearrange("p c t -> p (c t)"),
            )

        def scores(b):
            att = next_bank([P, HEADS, HEAD_DIM])
            for g in range(HEADS):
                q_cols = slice(g * HEAD_DIM, (g + 1) * HEAD_DIM)
                k_cols = slice(SIDE_COLS + g * HEAD_DIM, SIDE_COLS + (g + 1) * HEAD_DIM)
                nc.tensor.matmul_mx(
                    out=att[:, g, :],
                    lhsT=qk_codes[:, b, q_cols].bitcast(FP8X4),
                    lhsT_scale=qk_scales[:, b, q_cols],
                    rhs=qk_codes[:, b, k_cols].bitcast(FP8X4),
                    rhs_scale=qk_scales[:, b, k_cols],
                    start=True,
                    stop=True,
                )
            top = sbuf_ring("top", b, 5, [P, HEADS], F32)
            nc.vector.tensor_reduce(out=top[:], in_=att[:], axis=mybir.AxisListType.X, op=ALU.max)
            shift = sbuf_ring("shift", b, 5, [P, HEADS], F32)
            nc.gpsimd.tensor_scalar(
                out=shift[:], in0=top[:], scalar1=-SOFTMAX_SCALE, scalar2=0.0, op0=ALU.mult, op1=ALU.add
            )
            return att, shift

        def exponentials(att, shift, b):
            weights = sbuf_ring("weights", b, 6, [P, HEADS, HEAD_DIM], F32)
            total = sbuf_ring("total", b, 4, [P, HEADS], F32)
            for g in range(HEADS):
                nc.scalar.activation(
                    out=weights[:, g, :],
                    in_=att[:, g, :],
                    func=ACT.Exp,
                    scale=SOFTMAX_SCALE,
                    bias=shift[:, g : g + 1],
                    accum_out=total[:, g : g + 1],
                )
            return weights, total

        def invert_total(total, b):
            inv_total = sbuf_ring("inv_total", b, 4, [P, HEADS], F32)
            nc.vector.reciprocal(out=inv_total[:], in_=total[:])
            return inv_total

        def divide_on_gpsimd(weights, inv_total):
            for g in range(HEADS // 2):
                nc.gpsimd.tensor_scalar(
                    out=weights[:, g, :],
                    in0=weights[:, g, :],
                    scalar1=inv_total[:, g : g + 1],
                    scalar2=0.0,
                    op0=ALU.mult,
                    op1=ALU.add,
                )

        def divide_on_scalar(weights, inv_total):
            for g in range(HEADS // 2, HEADS):
                nc.scalar.activation(
                    out=weights[:, g, :], in_=weights[:, g, :], func=ACT.Copy, scale=inv_total[:, g : g + 1]
                )

        def store(weights, b):
            nc.sync.dma_start(out=out[b].rearrange("g d e -> d g e"), in_=weights[:])

        token_rows = {0: load_token_rows(0, 2)}
        weight_rows = [load_weight_rows(0, 2), load_weight_rows(1, 1)]
        nc.sync.dma_start(out=gains[:, 0, :], in_=w_q_norm.partition_broadcast(P))
        nc.sync.dma_start(out=gains[:, 1, :], in_=w_k_norm.partition_broadcast(P))
        for b in (1, 2):
            token_rows[b] = load_token_rows(b, 1)

        both_engines = (nc.scalar.copy, nc.vector.tensor_copy)
        scalar_alone = (nc.scalar.copy, nc.scalar.copy)
        vector_alone = (nc.vector.tensor_copy, nc.vector.tensor_copy)
        token_codes = {0: new_token_codes(0)}
        grouped_rows = gather_words(transpose_rows(token_rows[0]), 0, both_engines)
        quantise_rows(grouped_rows[:], token_codes[0][0][:], token_codes[0][1][:])
        half = SIDE_COLS // 2
        grouped_rows = gather_words(transpose_rows(weight_rows[0]), 1, scalar_alone)
        for i in range(2):
            cols = slice(i * half, (i + 1) * half)
            quantise_rows(grouped_rows[:, i * half * PACK : (i + 1) * half * PACK], w_codes[:, cols], w_scales[:, cols])
        side_cols = slice(SIDE_COLS, QK_COLS)
        grouped_rows = gather_words(transpose_rows(weight_rows[1]), 2, vector_alone)
        quantise_rows(grouped_rows[:], w_codes[:, side_cols], w_scales[:, side_cols])

        pairs = BATCH * GROUPS // 2
        batch_pairs = GROUPS // 2
        sums, sumsq, inv_rms, rows, grouped_qk = {}, {}, {}, {}, {}
        for s in range(pairs + 1):
            b, step = divmod(s, batch_pairs)
            if s == 1:
                turned = transpose_rows(token_rows[1])
            if s == 2 or (step == 0 and 1 <= b < BATCH - 1):
                grouped_rows = gather_words(turned, b + 1, scalar_alone)
            if s < pairs:
                sumsq[s] = sbuf_ring("sumsq", s, 4, [P, 2, TOKEN_TILES], F32)
                inv_rms[s] = sbuf_ring("inv_rms", s, 4, [P, 2, TOKEN_TILES], F32)
            for i in range(2):
                if s < pairs:
                    unit = 2 * s + i
                    sums[unit] = project(token_codes[b][0], token_codes[b][1], unit % GROUPS)
                    sum_squares(sums[unit], unit, sumsq[s])
                if s == 0:
                    inverse_rms(inv_rms[0][:, i, :], sumsq[0][:, i, :])
                elif i == 0 and s >= 2:
                    inverse_rms(inv_rms[s - 1][:], sumsq[s - 1][:])
            if step == batch_pairs - 1 and b + 2 < BATCH:
                turned = transpose_rows(token_rows[b + 2])
                if b + 3 < BATCH:
                    token_rows[b + 3] = load_token_rows(b + 3, 1)
            if s == pairs - 1:
                waiting = {0: scores(0)}
            if s >= 1:
                done_b, done_step = divmod(s - 1, batch_pairs)
                if done_step == 0:
                    rows[done_b] = sbuf_ring("rows_qk", done_b, 2, [P, TOKEN_TILES, QK_COLS], BF16)
                    grouped_qk[done_b] = sbuf_ring("grouped_qk", done_b, DEFERRED, [P, QK_COLS, PACK], BF16)
                normalise(sums[2 * s - 2], inv_rms[s - 1], 2 * s - 2, rows[done_b], range(TOKEN_TILES))
                normalise(sums[2 * s - 1], inv_rms[s - 1], 2 * s - 1, rows[done_b], range(TOKEN_TILES - 1))
                if done_step == 1 and done_b + 1 < BATCH:
                    token_codes[done_b + 1] = new_token_codes(done_b + 1)
                    quantise_rows(grouped_rows[:], token_codes[done_b + 1][0][:], token_codes[done_b + 1][1][:])
                if done_step == 1 and 1 <= done_b <= BATCH - DEFERRED:
                    quantise_qk(grouped_qk[done_b - 1], done_b - 1)
                normalise(sums[2 * s - 1], inv_rms[s - 1], 2 * s - 1, rows[done_b], range(TOKEN_TILES - 1, TOKEN_TILES))
            if s == pairs:
                waiting[1] = scores(1)
            if s >= 1:
                last_keys = done_b == BATCH - 1 and done_step >= 2
                if last_keys or done_step % 2 == 1:
                    pairs_at_once = 1 if last_keys else 2
                    end = 2 * (done_step + 1) * HEAD_DIM
                    interleave(rows[done_b], grouped_qk[done_b], slice(end - 2 * pairs_at_once * HEAD_DIM, end))

        waiting[2] = scores(2)
        for b in range(BATCH):
            if b + 3 < BATCH:
                waiting[b + 3] = scores(b + 3)
            weights, total = exponentials(waiting[b][0], waiting[b][1], b)
            inv_total = invert_total(total, b)
            divide_on_gpsimd(weights, inv_total)
            if b > 0:
                divide_on_scalar(last_weights, last_inv_total)
                store(last_weights, b - 1)
            last_weights, last_inv_total = weights, inv_total
            if b % 3 == 1 and b < 3 * DEFERRED:
                deferred_b = BATCH - DEFERRED + b // 3
                quantise_qk(grouped_qk[deferred_b], deferred_b)
        divide_on_scalar(last_weights, last_inv_total)
        store(last_weights, BATCH - 1)
